import numpy as np
import ml_dtypes


def mxq(x, axis, fmt="e4m3"):
    dtype, down = {"e4m3": (ml_dtypes.float8_e4m3fn, 7), "e5m2": (ml_dtypes.float8_e5m2, 14)}[fmt]
    v = np.moveaxis(np.asarray(x, np.float32).astype(ml_dtypes.bfloat16).astype(np.float64), axis, -1)
    blocks = v.reshape(v.shape[:-1] + (-1, 32))
    amax = np.abs(blocks).max(-1, keepdims=True)
    byte = np.maximum(np.where(amax > 0, np.frexp(amax)[1] - 1 + 127, 0) - down, 1)
    scale = np.exp2(byte - 127.0)
    codes = (blocks / scale).astype(np.float32).astype(dtype).astype(np.float64)
    return np.moveaxis((codes * scale).reshape(v.shape), -1, axis)


WIDE = False


def mx_kscale(k):
    if not WIDE:
        return np.ones(k)
    levels = np.array([10, -10, 5, -5, 0])
    a = np.random.permutation(np.resize(levels, k // 512 * 4)).reshape(k // 512, 4)
    idx = np.arange(k)
    return np.exp2(a[idx // 512, idx % 128 // 32])


BF16 = ml_dtypes.bfloat16


def bf(x):
    return np.asarray(x, np.float32).astype(BF16)


def f64(x):
    return np.asarray(x).astype(np.float64)


E2M1 = np.array([0.0, 0.5, 1.0, 1.5, 2.0, 3.0, 4.0, 6.0, -0.0, -0.5, -1.0, -1.5, -2.0, -3.0, -4.0, -6.0])


def pack_weight(w, fmt):
    k, n = w.shape
    w = f64(bf(w)).reshape(k // 32, 32, n)
    amax = np.abs(w).max(1)
    if fmt == "e4m3":
        byte = np.frexp(amax)[1] - 1 + 127 - 7
    else:
        mant, ex = np.frexp(amax / 6.0)
        byte = np.where(mant > 0.5, ex, ex - 1) + 127
    byte = np.clip(np.where(amax > 0, byte, 1), 1, 254)
    scaled = (w * np.exp2(127.0 - byte)[:, None, :]).reshape(k, n).astype(np.float32)
    by_word = np.ascontiguousarray(scaled.reshape(k // 512, 128, 4, n).transpose(0, 1, 3, 2))
    if fmt == "e4m3":
        words = by_word.astype(ml_dtypes.float8_e4m3fn).view(np.uint8)
    else:
        c = by_word.astype(ml_dtypes.float4_e2m1fn).view(np.uint8) & 0xF
        words = c[..., 0::2] | (c[..., 1::2] << 4)
    return np.ascontiguousarray(words), np.ascontiguousarray(byte.astype(np.uint8).reshape(k // 512, 16, n))


def unpack_weight(words, scales, fmt):
    g, p, n, _ = words.shape
    if fmt == "e4m3":
        vals = np.ascontiguousarray(words).view(ml_dtypes.float8_e4m3fn).astype(np.float64)
    else:
        nib = np.empty((g, p, n, 4), np.uint8)
        nib[..., 0::2] = words & 0xF
        nib[..., 1::2] = words >> 4
        vals = E2M1[nib]
    vals = vals * np.repeat(np.exp2(scales.astype(np.float64) - 127.0), 8, axis=1)[..., None]
    return vals.transpose(0, 1, 3, 2).reshape(g * 512, n)


B, D, H = 512, 1024, 1024
PASS = 512
MX_REC = H % PASS == 0


def sigmoid(v):
    return 1.0 / (1.0 + np.exp(-v))


def setup_inputs():
    s = mx_kscale(D)
    r = mx_kscale(H) if MX_REC else np.ones(H)
    gate_b = np.concatenate([np.zeros(H), np.zeros(H), np.ones(H), np.zeros(H)])
    x_t = bf(np.random.standard_normal((B, D)) * s)
    h_prev = bf(np.random.standard_normal((B, H)) * r)
    c_prev = bf(np.random.standard_normal((B, H)))
    n_prev = bf(0.5 + np.abs(np.random.standard_normal((B, H))))
    W_words, W_scales = pack_weight(np.random.standard_normal((D, 4 * H)) / np.sqrt(D) / s[:, None], "e4m3")
    R_words, R_scales = pack_weight(np.random.standard_normal((H, 4 * H)) / np.sqrt(H) / r[:, None], "e4m3")
    b = bf(gate_b + 0.2 * np.random.standard_normal(4 * H))
    return {"x_t": x_t,
            "h_prev": h_prev,
            "c_prev": c_prev,
            "n_prev": n_prev,
            "W_words": W_words,
            "W_scales": W_scales,
            "R_words": R_words,
            "R_scales": R_scales,
            "b": b}


def reference(x_t, h_prev, c_prev, n_prev, W_words, W_scales, R_words, R_scales, b):
    inp = mxq(f64(x_t), 1, "e4m3") @ unpack_weight(W_words, W_scales, "e4m3")
    if MX_REC:
        rec = mxq(f64(h_prev), 1, "e4m3") @ unpack_weight(R_words, R_scales, "e4m3")
    else:
        rec = f64(h_prev) @ unpack_weight(R_words, R_scales, "e4m3")
    pre = inp + rec + f64(b)
    z_tilde, i_tilde, f_tilde, o_tilde = np.split(pre, 4, axis=-1)
    z_t = np.tanh(z_tilde)
    i_t = np.minimum(np.exp(i_tilde), 50.0)
    f_t = sigmoid(f_tilde)
    o_t = sigmoid(o_tilde)
    c_t = f_t * f64(c_prev) + i_t * z_t
    n_t = f_t * f64(n_prev) + i_t
    h_t = o_t * (c_t / (n_t + 1e-6))
    return h_t, c_t, n_t

@@ -1,0 +1,185 @@
+from contextlib import ExitStack
+
+import concourse.mybir as mybir
+from concourse.masks import make_identity
+
+FP8X4 = mybir.dt.float8_e4m3fn_x4
+BF16 = mybir.dt.bfloat16
+F32 = mybir.dt.float32
+I32 = mybir.dt.int32
+U32 = mybir.dt.uint32
+U8 = mybir.dt.uint8
+ACT = mybir.ActivationFunctionType
+ALU = mybir.AluOpType
+
+P = 128
+BATCH = 512
+HIDDEN = 1024
+K_PASS = 512
+PASSES = 4
+ROW_TILES = BATCH // P
+BLOCK = 512
+BLOCKS = HIDDEN // BLOCK
+GATE_Z, GATE_I, GATE_F, GATE_O = 0, 1, 2, 3
+EPS = 1e-6
+I_MAX = 50.0
+
+FLOPS = 2 * BATCH * (2 * HIDDEN) * (4 * HIDDEN)
+
+
+def tile_slstmcell_kernel(
+    tc, x_t, h_prev, c_prev, n_prev, W_words, W_scales, R_words, R_scales, b, h_out, c_out, n_out
+):
+    nc = tc.nc
+    with ExitStack() as ctx:
+        ctx.enter_context(tc.manual_schedule())
+        keep = ctx.enter_context(tc.tile_pool(name="keep", bufs=1))
+        psum = ctx.enter_context(tc.psum_pool(name="psum", bufs=8))
+
+        w_codes = keep.tile([P, PASSES, 4 * HIDDEN], U32, align_bytes=64)
+        a_codes = keep.tile([P, PASSES, BATCH], U32, align_bytes=64)
+        w_planes = keep.tile([P, 4 * HIDDEN], U8, align_bytes=64)
+        a_planes = keep.tile([P, PASSES, BATCH], U8, align_bytes=64)
+        bias_rows = keep.tile([P, 4 * HIDDEN], BF16)
+        c_old = keep.tile([P, ROW_TILES, HIDDEN], BF16)
+        n_old = keep.tile([P, ROW_TILES, HIDDEN], BF16)
+        n_half = keep.tile([P, ROW_TILES, HIDDEN], BF16)
+        identity = keep.tile([P, P], F32)
+        eps = keep.tile([P, 1], F32)
+
+        nc.vector.memset(w_planes[:].bitcast(I32), 0)
+        nc.vector.memset(eps[:], EPS)
+        make_identity(nc, identity[:])
+
+        def row_tiled(dram):
+            return dram.rearrange("(t p) d -> p t d", p=P)
+
+        def load_weight_block(gate, block):
+            first = gate * HIDDEN + block * BLOCK
+            for operand, words in enumerate((W_words, R_words)):
+                nc.sync.dma_start(
+                    out=w_codes[:, 2 * operand : 2 * operand + 2, first : first + BLOCK].bitcast(I32),
+                    in_=words.rearrange("g p n t -> p g (n t)")[:, :, 4 * first : 4 * (first + BLOCK)].bitcast(I32),
+                )
+
+        with tc.tile_pool(name="stage", bufs=1) as stage:
+            x_raw = stage.tile([P, ROW_TILES, HIDDEN], BF16)
+            h_raw = stage.tile([P, ROW_TILES, HIDDEN], BF16)
+            for raw, dram in ((x_raw, x_t), (h_raw, h_prev)):
+                for t in range(ROW_TILES):
+                    nc.sync.dma_start(out=raw[:, t, :], in_=row_tiled(dram)[:, t, :])
+            for quadrant in range(4):
+                for operand, scales in enumerate((W_scales, R_scales)):
+                    first = 32 * quadrant + 8 * operand
+                    nc.sync.dma_start(
+                        out=w_planes[first : first + 8, :].bitcast(I32),
+                        in_=scales[:, 4 * quadrant : 4 * quadrant + 4, :].bitcast(I32),
+                    )
+            nc.sync.dma_start(out=bias_rows[:], in_=b.partition_broadcast(P))
+            load_weight_block(GATE_I, 0)
+            load_weight_block(GATE_Z, 0)
+            load_weight_block(GATE_F, 0)
+            nc.sync.dma_start(out=n_old[:], in_=row_tiled(n_prev))
+            nc.sync.dma_start(out=c_old[:], in_=row_tiled(c_prev))
+            load_weight_block(GATE_O, 0)
+            for block in range(1, BLOCKS):
+                for gate in (GATE_I, GATE_Z, GATE_F, GATE_O):
+                    load_weight_block(gate, block)
+
+            grouped = stage.tile([P, PASSES, BATCH, 4], BF16, align_bytes=64)
+            grouped_words = grouped[:].bitcast(F32)
+            for operand, raw in enumerate((x_raw, h_raw)):
+                for t in range(ROW_TILES):
+                    words = raw[:, t, :].bitcast(F32)
+                    bank = psum.tile([P, BLOCK], F32, tag="bank")
+                    flipped = bank[:].rearrange("p (g u r) -> p g u r", g=2, u=2)
+                    for g in range(2):
+                        for u in range(2):
+                            nc.tensor.transpose(flipped[:, g, u, :], words[:, 256 * g + u : 256 * (g + 1) : 2], identity[:])
+                    target = grouped_words[:, 2 * operand : 2 * operand + 2, t * P : (t + 1) * P, :]
+                    source = flipped.rearrange("p g u r -> p g r u")
+                    if operand == 0:
+                        nc.vector.tensor_copy(out=target, in_=source)
+                    else:
+                        nc.scalar.copy(out=target, in_=source)
+            for s in range(PASSES):
+                nc.vector.quantize_mx(
+                    out=a_codes[:, s, :].bitcast(FP8X4),
+                    scales=a_planes[:, s, :],
+                    in_=grouped[:, s, :, :].rearrange("p r t -> p (r t)"),
+                )
+
+        gates = ctx.enter_context(tc.tile_pool(name="gates", bufs=ROW_TILES))
+        results = ctx.enter_context(tc.tile_pool(name="results", bufs=2 * ROW_TILES))
+
+        def gate_block(gate, block, t, func, scale, name):
+            first = gate * HIDDEN + block * BLOCK
+            cols = slice(first, first + BLOCK)
+            rows = slice(t * P, (t + 1) * P)
+            acc = psum.tile([P, BLOCK], F32, tag="bank")
+            for s in range(PASSES):
+                nc.tensor.matmul_mx(
+                    out=acc[:],
+                    lhsT=a_codes[:, s, rows].bitcast(FP8X4),
+                    lhsT_scale=a_planes[:, s, rows],
+                    rhs=w_codes[:, s, cols].bitcast(FP8X4),
+                    rhs_scale=w_planes[4 * s : P, cols],
+                    start=(s == 0),
+                    stop=(s == PASSES - 1),
+                )
+            value = gates.tile([P, BLOCK], F32, name=name)
+            nc.vector.tensor_tensor(out=value[:], in0=acc[:], in1=bias_rows[:, cols], op=ALU.add)
+            nc.scalar.activation(out=value[:], in_=value[:], func=func, scale=scale)
+            return value
+
+        tiles = range(ROW_TILES)
+        for block in range(BLOCKS):
+            cols = slice(block * BLOCK, (block + 1) * BLOCK)
+            exp_i = [gate_block(GATE_I, block, t, ACT.Exp, 1.0, "exp_i") for t in tiles]
+            z = [gate_block(GATE_Z, block, t, ACT.Tanh, 1.0, "z") for t in tiles]
+            iz = []
+            for t in tiles:
+                product = gates.tile([P, BLOCK], F32, name="iz")
+                nc.vector.scalar_tensor_tensor(
+                    out=product[:], in0=exp_i[t][:], scalar=I_MAX, in1=z[t][:], op0=ALU.min, op1=ALU.mult
+                )
+                iz.append(product)
+            tanh_f = [gate_block(GATE_F, block, t, ACT.Tanh, 0.5, "tanh_f") for t in tiles]
+            tanh_o = [gate_block(GATE_O, block, t, ACT.Tanh, 0.5, "tanh_o") for t in tiles]
+            if block == 0:
+                nc.vector.tensor_scalar_mul(out=n_half[:], in0=n_old[:], scalar1=0.5)
+
+            c_new, n_new, h_new, inverse = [], [], [], []
+            for t in tiles:
+                c_new.append(results.tile([P, BLOCK], F32, name="c_new"))
+                n_new.append(results.tile([P, BLOCK], F32, name="n_new"))
+                nc.vector.scalar_tensor_tensor(
+                    out=c_new[t][:], in0=tanh_f[t][:], scalar=1.0, in1=c_old[:, t, cols], op0=ALU.add, op1=ALU.mult
+                )
+                nc.vector.scalar_tensor_tensor(
+                    out=n_new[t][:], in0=tanh_f[t][:], scalar=1.0, in1=n_half[:, t, cols], op0=ALU.add, op1=ALU.mult
+                )
+            for t in tiles:
+                rows = slice(t * P, (t + 1) * P)
+                nc.vector.scalar_tensor_tensor(
+                    out=c_new[t][:], in0=c_new[t][:], scalar=0.5, in1=iz[t][:], op0=ALU.mult, op1=ALU.add
+                )
+                nc.vector.scalar_tensor_tensor(
+                    out=n_new[t][:], in0=exp_i[t][:], scalar=I_MAX, in1=n_new[t][:], op0=ALU.min, op1=ALU.add
+                )
+                nc.sync.dma_start(out=c_out[rows, cols], in_=c_new[t][:])
+                nc.sync.dma_start(out=n_out[rows, cols], in_=n_new[t][:])
+                inverse.append(gates.tile([P, BLOCK], F32, name="inverse"))
+                nc.scalar.activation(out=inverse[t][:], in_=n_new[t][:], func=ACT.Ln, bias=eps[:])
+            for t in tiles:
+                h_new.append(results.tile([P, BLOCK], F32, name="h_new"))
+                nc.vector.scalar_tensor_tensor(
+                    out=h_new[t][:], in0=tanh_o[t][:], scalar=1.0, in1=c_new[t][:], op0=ALU.add, op1=ALU.mult
+                )
+                nc.scalar.activation(out=inverse[t][:], in_=inverse[t][:], func=ACT.Exp, scale=-1.0)
+            for t in tiles:
+                rows = slice(t * P, (t + 1) * P)
+                nc.vector.scalar_tensor_tensor(
+                    out=h_new[t][:], in0=h_new[t][:], scalar=0.5, in1=inverse[t][:], op0=ALU.mult, op1=ALU.mult
+                )
+                nc.sync.dma_start(out=h_out[rows, cols], in_=h_new[t][:])

@@ -15,14 +15,15 @@ ALU = mybir.AluOpType
 P = 128
 BATCH = 512
 HIDDEN = 1024
-K_PASS = 512
 PASSES = 4
 ROW_TILES = BATCH // P
 BLOCK = 512
 BLOCKS = HIDDEN // BLOCK
+COL_TILES = BLOCK // P
 GATE_Z, GATE_I, GATE_F, GATE_O = 0, 1, 2, 3
 EPS = 1e-6
 I_MAX = 50.0
+SPREAD = 32
 
 FLOPS = 2 * BATCH * (2 * HIDDEN) * (4 * HIDDEN)
 
@@ -31,6 +32,7 @@ def tile_slstmcell_kernel(
     tc, x_t, h_prev, c_prev, n_prev, W_words, W_scales, R_words, R_scales, b, h_out, c_out, n_out
 ):
     nc = tc.nc
+    tiles = range(ROW_TILES)
     with ExitStack() as ctx:
         ctx.enter_context(tc.manual_schedule())
         keep = ctx.enter_context(tc.tile_pool(name="keep", bufs=1))
@@ -40,7 +42,10 @@ def tile_slstmcell_kernel(
         a_codes = keep.tile([P, PASSES, BATCH], U32, align_bytes=64)
         w_planes = keep.tile([P, 4 * HIDDEN], U8, align_bytes=64)
         a_planes = keep.tile([P, PASSES, BATCH], U8, align_bytes=64)
+        b_row = keep.tile([P, 4 * HIDDEN], BF16)
+        ones = keep.tile([P, P], BF16)
         bias_rows = keep.tile([P, 4 * HIDDEN], BF16)
+        bias_cols = keep.tile([P, 4 * HIDDEN // P], F32)
         c_old = keep.tile([P, ROW_TILES, HIDDEN], BF16)
         n_old = keep.tile([P, ROW_TILES, HIDDEN], BF16)
         n_half = keep.tile([P, ROW_TILES, HIDDEN], BF16)
@@ -48,6 +53,8 @@ def tile_slstmcell_kernel(
         eps = keep.tile([P, 1], F32)
 
         nc.vector.memset(w_planes[:].bitcast(I32), 0)
+        nc.vector.memset(b_row[:].bitcast(I32), 0)
+        nc.vector.memset(ones[:], 1.0)
         nc.vector.memset(eps[:], EPS)
         make_identity(nc, identity[:])
 
@@ -66,8 +73,9 @@ def tile_slstmcell_kernel(
             x_raw = stage.tile([P, ROW_TILES, HIDDEN], BF16)
             h_raw = stage.tile([P, ROW_TILES, HIDDEN], BF16)
             for raw, dram in ((x_raw, x_t), (h_raw, h_prev)):
-                for t in range(ROW_TILES):
+                for t in tiles:
                     nc.sync.dma_start(out=raw[:, t, :], in_=row_tiled(dram)[:, t, :])
+            nc.sync.dma_start(out=b_row[0:1, :], in_=b.rearrange("(o n) -> o n", o=1))
             for quadrant in range(4):
                 for operand, scales in enumerate((W_scales, R_scales)):
                     first = 32 * quadrant + 8 * operand
@@ -75,7 +83,6 @@ def tile_slstmcell_kernel(
                         out=w_planes[first : first + 8, :].bitcast(I32),
                         in_=scales[:, 4 * quadrant : 4 * quadrant + 4, :].bitcast(I32),
                     )
-            nc.sync.dma_start(out=bias_rows[:], in_=b.partition_broadcast(P))
             load_weight_block(GATE_I, 0)
             load_weight_block(GATE_Z, 0)
             load_weight_block(GATE_F, 0)
@@ -89,7 +96,7 @@ def tile_slstmcell_kernel(
             grouped = stage.tile([P, PASSES, BATCH, 4], BF16, align_bytes=64)
             grouped_words = grouped[:].bitcast(F32)
             for operand, raw in enumerate((x_raw, h_raw)):
-                for t in range(ROW_TILES):
+                for t in tiles:
                     words = raw[:, t, :].bitcast(F32)
                     bank = psum.tile([P, BLOCK], F32, tag="bank")
                     flipped = bank[:].rearrange("p (g u r) -> p g u r", g=2, u=2)
@@ -109,47 +116,99 @@ def tile_slstmcell_kernel(
                     in_=grouped[:, s, :, :].rearrange("p r t -> p (r t)"),
                 )
 
+        for first in range(GATE_I * HIDDEN, (GATE_F + 1) * HIDDEN, BLOCK):
+            repeated = psum.tile([P, BLOCK], F32, tag="bank")
+            nc.tensor.matmul(out=repeated[:], lhsT=ones[:], rhs=b_row[:, first : first + BLOCK], start=True, stop=True)
+            nc.scalar.copy(out=bias_rows[:, first : first + BLOCK], in_=repeated[:])
+        stood_up = psum.tile([P, BLOCK], F32, tag="bank")
+        stood_up_tiles = stood_up[:].rearrange("p (m n) -> p m n", n=SPREAD)
+        per_gate = HIDDEN // P
+        for slot, gate in enumerate((GATE_Z, GATE_O)):
+            for j in range(per_gate):
+                first = gate * HIDDEN + j * P
+                nc.tensor.matmul(
+                    out=stood_up_tiles[:, slot * per_gate + j, :],
+                    lhsT=b_row[:, first : first + P],
+                    rhs=ones[:, 0:SPREAD],
+                    start=True,
+                    stop=True,
+                )
+        nc.vector.tensor_copy(
+            out=bias_cols[:, GATE_Z * per_gate : (GATE_Z + 1) * per_gate], in_=stood_up_tiles[:, 0:per_gate, 0]
+        )
+        nc.vector.tensor_scalar_mul(
+            out=bias_cols[:, GATE_O * per_gate : (GATE_O + 1) * per_gate],
+            in0=stood_up_tiles[:, per_gate : 2 * per_gate, 0],
+            scalar1=0.5,
+        )
+
         gates = ctx.enter_context(tc.tile_pool(name="gates", bufs=ROW_TILES))
         results = ctx.enter_context(tc.tile_pool(name="results", bufs=2 * ROW_TILES))
 
-        def gate_block(gate, block, t, func, scale, name):
+        def gate_by_rows(gate, block, func, scale, name):
             first = gate * HIDDEN + block * BLOCK
             cols = slice(first, first + BLOCK)
-            rows = slice(t * P, (t + 1) * P)
-            acc = psum.tile([P, BLOCK], F32, tag="bank")
-            for s in range(PASSES):
-                nc.tensor.matmul_mx(
-                    out=acc[:],
-                    lhsT=a_codes[:, s, rows].bitcast(FP8X4),
-                    lhsT_scale=a_planes[:, s, rows],
-                    rhs=w_codes[:, s, cols].bitcast(FP8X4),
-                    rhs_scale=w_planes[4 * s : P, cols],
-                    start=(s == 0),
-                    stop=(s == PASSES - 1),
-                )
-            value = gates.tile([P, BLOCK], F32, name=name)
-            nc.vector.tensor_tensor(out=value[:], in0=acc[:], in1=bias_rows[:, cols], op=ALU.add)
-            nc.scalar.activation(out=value[:], in_=value[:], func=func, scale=scale)
-            return value
+            values = []
+            for t in tiles:
+                rows = slice(t * P, (t + 1) * P)
+                acc = psum.tile([P, BLOCK], F32, tag="bank")
+                for s in range(PASSES):
+                    nc.tensor.matmul_mx(
+                        out=acc[:],
+                        lhsT=a_codes[:, s, rows].bitcast(FP8X4),
+                        lhsT_scale=a_planes[:, s, rows],
+                        rhs=w_codes[:, s, cols].bitcast(FP8X4),
+                        rhs_scale=w_planes[4 * s : P, cols],
+                        start=(s == 0),
+                        stop=(s == PASSES - 1),
+                    )
+                value = gates.tile([P, BLOCK], F32, name=name)
+                nc.vector.tensor_tensor(out=value[:], in0=acc[:], in1=bias_rows[:, cols], op=ALU.add)
+                nc.scalar.activation(out=value[:], in_=value[:], func=func, scale=scale)
+                values.append(value)
+            return values
 
-        tiles = range(ROW_TILES)
+        def gate_by_columns(gate, block, scale, name):
+            values = []
+            for j in range(COL_TILES):
+                first = gate * HIDDEN + block * BLOCK + j * P
+                cols = slice(first, first + P)
+                acc = psum.tile([P, BATCH], F32, tag="bank")
+                for s in range(PASSES):
+                    nc.tensor.matmul_mx(
+                        out=acc[:],
+                        lhsT=w_codes[:, s, cols].bitcast(FP8X4),
+                        lhsT_scale=w_planes[4 * s : P, cols],
+                        rhs=a_codes[:, s, :].bitcast(FP8X4),
+                        rhs_scale=a_planes[:, s, :],
+                        start=(s == 0),
+                        stop=(s == PASSES - 1),
+                    )
+                value = gates.tile([P, BATCH], F32, name=name)
+                nc.scalar.activation(
+                    out=value[:], in_=acc[:], func=ACT.Tanh, bias=bias_cols[:, first // P : first // P + 1], scale=scale
+                )
+                values.append(value)
+            return values
+
+        def rows_onto_partitions(values, name):
+            banks = [psum.tile([P, BLOCK], F32, tag="bank", name=name) for t in tiles]
+            for j, value in enumerate(values):
+                for t in tiles:
+                    nc.tensor.transpose(banks[t][:, j * P : (j + 1) * P], value[:, t * P : (t + 1) * P], identity[:])
+            return banks
+
+        exp_i = gate_by_rows(GATE_I, 0, ACT.Exp, 1.0, "exp_i")
         for block in range(BLOCKS):
             cols = slice(block * BLOCK, (block + 1) * BLOCK)
-            exp_i = [gate_block(GATE_I, block, t, ACT.Exp, 1.0, "exp_i") for t in tiles]
-            z = [gate_block(GATE_Z, block, t, ACT.Tanh, 1.0, "z") for t in tiles]
-            iz = []
-            for t in tiles:
-                product = gates.tile([P, BLOCK], F32, name="iz")
-                nc.vector.scalar_tensor_tensor(
-                    out=product[:], in0=exp_i[t][:], scalar=I_MAX, in1=z[t][:], op0=ALU.min, op1=ALU.mult
-                )
-                iz.append(product)
-            tanh_f = [gate_block(GATE_F, block, t, ACT.Tanh, 0.5, "tanh_f") for t in tiles]
-            tanh_o = [gate_block(GATE_O, block, t, ACT.Tanh, 0.5, "tanh_o") for t in tiles]
+            z_cols = gate_by_columns(GATE_Z, block, 1.0, "z_cols")
+            tanh_f = gate_by_rows(GATE_F, block, ACT.Tanh, 0.5, "tanh_f")
+            z = rows_onto_partitions(z_cols, "z")
+            tanh_o_cols = gate_by_columns(GATE_O, block, 0.5, "tanh_o_cols")
             if block == 0:
                 nc.vector.tensor_scalar_mul(out=n_half[:], in0=n_old[:], scalar1=0.5)
 
-            c_new, n_new, h_new, inverse = [], [], [], []
+            c_new, n_new, h_new, iz, inverse = [], [], [], [], []
             for t in tiles:
                 c_new.append(results.tile([P, BLOCK], F32, name="c_new"))
                 n_new.append(results.tile([P, BLOCK], F32, name="n_new"))
@@ -158,6 +217,11 @@ def tile_slstmcell_kernel(
                 )
                 nc.vector.scalar_tensor_tensor(
                     out=n_new[t][:], in0=tanh_f[t][:], scalar=1.0, in1=n_half[:, t, cols], op0=ALU.add, op1=ALU.mult
+                )
+            for t in tiles:
+                iz.append(gates.tile([P, BLOCK], F32, name="iz"))
+                nc.vector.scalar_tensor_tensor(
+                    out=iz[t][:], in0=exp_i[t][:], scalar=I_MAX, in1=z[t][:], op0=ALU.min, op1=ALU.mult
                 )
             for t in tiles:
                 rows = slice(t * P, (t + 1) * P)
@@ -172,11 +236,15 @@ def tile_slstmcell_kernel(
                 inverse.append(gates.tile([P, BLOCK], F32, name="inverse"))
                 nc.scalar.activation(out=inverse[t][:], in_=n_new[t][:], func=ACT.Ln, bias=eps[:])
             for t in tiles:
+                nc.scalar.activation(out=inverse[t][:], in_=inverse[t][:], func=ACT.Exp, scale=-1.0)
+            if block + 1 < BLOCKS:
+                exp_i = gate_by_rows(GATE_I, block + 1, ACT.Exp, 1.0, "exp_i")
+            tanh_o = rows_onto_partitions(tanh_o_cols, "tanh_o")
+            for t in tiles:
                 h_new.append(results.tile([P, BLOCK], F32, name="h_new"))
                 nc.vector.scalar_tensor_tensor(
                     out=h_new[t][:], in0=tanh_o[t][:], scalar=1.0, in1=c_new[t][:], op0=ALU.add, op1=ALU.mult
                 )
-                nc.scalar.activation(out=inverse[t][:], in_=inverse[t][:], func=ACT.Exp, scale=-1.0)
             for t in tiles:
                 rows = slice(t * P, (t + 1) * P)
                 nc.vector.scalar_tensor_tensor(

@@ -37,20 +37,24 @@ def tile_slstmcell_kernel(
         ctx.enter_context(tc.manual_schedule())
         keep = ctx.enter_context(tc.tile_pool(name="keep", bufs=1))
         psum = ctx.enter_context(tc.psum_pool(name="psum", bufs=8))
+        gates = ctx.enter_context(tc.tile_pool(name="gates", bufs=ROW_TILES))
+        results = ctx.enter_context(tc.tile_pool(name="results", bufs=ROW_TILES))
+        stage = ctx.enter_context(tc.tile_pool(name="stage", bufs=1))
 
         w_codes = keep.tile([P, PASSES, 4 * HIDDEN], U32, align_bytes=64)
         a_codes = keep.tile([P, PASSES, BATCH], U32, align_bytes=64)
         w_planes = keep.tile([P, 4 * HIDDEN], U8, align_bytes=64)
         a_planes = keep.tile([P, PASSES, BATCH], U8, align_bytes=64)
-        b_row = keep.tile([P, 4 * HIDDEN], BF16)
-        ones = keep.tile([P, P], BF16)
-        bias_rows = keep.tile([P, 4 * HIDDEN], BF16)
-        bias_cols = keep.tile([P, 4 * HIDDEN // P], F32)
         c_old = keep.tile([P, ROW_TILES, HIDDEN], BF16)
         n_old = keep.tile([P, ROW_TILES, HIDDEN], BF16)
         n_half = keep.tile([P, ROW_TILES, HIDDEN], BF16)
         identity = keep.tile([P, P], F32)
         eps = keep.tile([P, 1], F32)
+        b_row = stage.tile([P, 4 * HIDDEN], BF16)
+        ones = stage.tile([P, P], BF16)
+        x_raw = stage.tile([P, ROW_TILES, HIDDEN], BF16)
+        h_raw = stage.tile([P, ROW_TILES, HIDDEN], BF16)
+        grouped = stage.tile([P, PASSES, BATCH, 4], BF16, align_bytes=64)
 
         nc.vector.memset(w_planes[:].bitcast(I32), 0)
         nc.vector.memset(b_row[:].bitcast(I32), 0)
@@ -61,6 +65,10 @@ def tile_slstmcell_kernel(
         def row_tiled(dram):
             return dram.rearrange("(t p) d -> p t d", p=P)
 
+        def load_rows(t):
+            nc.sync.dma_start(out=x_raw[:, t, :], in_=row_tiled(x_t)[:, t, :])
+            nc.sync.dma_start(out=h_raw[:, t, :], in_=row_tiled(h_prev)[:, t, :])
+
         def load_weight_block(gate, block):
             first = gate * HIDDEN + block * BLOCK
             for operand, words in enumerate((W_words, R_words)):
@@ -69,110 +77,98 @@ def tile_slstmcell_kernel(
                     in_=words.rearrange("g p n t -> p g (n t)")[:, :, 4 * first : 4 * (first + BLOCK)].bitcast(I32),
                 )
 
-        with tc.tile_pool(name="stage", bufs=1) as stage:
-            x_raw = stage.tile([P, ROW_TILES, HIDDEN], BF16)
-            h_raw = stage.tile([P, ROW_TILES, HIDDEN], BF16)
-            for raw, dram in ((x_raw, x_t), (h_raw, h_prev)):
-                for t in tiles:
-                    nc.sync.dma_start(out=raw[:, t, :], in_=row_tiled(dram)[:, t, :])
-            nc.sync.dma_start(out=b_row[0:1, :], in_=b.rearrange("(o n) -> o n", o=1))
-            for quadrant in range(4):
-                for operand, scales in enumerate((W_scales, R_scales)):
-                    first = 32 * quadrant + 8 * operand
-                    nc.sync.dma_start(
-                        out=w_planes[first : first + 8, :].bitcast(I32),
-                        in_=scales[:, 4 * quadrant : 4 * quadrant + 4, :].bitcast(I32),
-                    )
-            load_weight_block(GATE_I, 0)
-            load_weight_block(GATE_Z, 0)
-            load_weight_block(GATE_F, 0)
-            nc.sync.dma_start(out=n_old[:], in_=row_tiled(n_prev))
-            nc.sync.dma_start(out=c_old[:], in_=row_tiled(c_prev))
-            load_weight_block(GATE_O, 0)
-            for block in range(1, BLOCKS):
-                for gate in (GATE_I, GATE_Z, GATE_F, GATE_O):
-                    load_weight_block(gate, block)
+        def load_state_block(block):
+            cols = slice(block * BLOCK, (block + 1) * BLOCK)
+            nc.sync.dma_start(out=n_old[:, :, cols], in_=row_tiled(n_prev)[:, :, cols])
+            nc.sync.dma_start(out=c_old[:, :, cols], in_=row_tiled(c_prev)[:, :, cols])
 
-            grouped = stage.tile([P, PASSES, BATCH, 4], BF16, align_bytes=64)
-            grouped_words = grouped[:].bitcast(F32)
+        for t in tiles:
+            load_rows(t)
+        for quadrant in range(4):
+            for operand, scales in enumerate((W_scales, R_scales)):
+                first = 32 * quadrant + 8 * operand
+                nc.sync.dma_start(
+                    out=w_planes[first : first + 8, :].bitcast(I32),
+                    in_=scales[:, 4 * quadrant : 4 * quadrant + 4, :].bitcast(I32),
+                )
+        nc.sync.dma_start(out=b_row[0:1, :], in_=b.rearrange("(o n) -> o n", o=1))
+        for block in range(BLOCKS):
+            load_weight_block(GATE_F, block)
+            load_state_block(block)
+            for gate in (GATE_I, GATE_Z, GATE_O):
+                load_weight_block(gate, block)
+
+        grouped_words = grouped[:].bitcast(F32)
+
+        def quantise_rows(t):
+            rows = slice(t * P, (t + 1) * P)
             for operand, raw in enumerate((x_raw, h_raw)):
-                for t in tiles:
-                    words = raw[:, t, :].bitcast(F32)
-                    bank = psum.tile([P, BLOCK], F32, tag="bank")
-                    flipped = bank[:].rearrange("p (g u r) -> p g u r", g=2, u=2)
-                    for g in range(2):
-                        for u in range(2):
-                            nc.tensor.transpose(flipped[:, g, u, :], words[:, 256 * g + u : 256 * (g + 1) : 2], identity[:])
-                    target = grouped_words[:, 2 * operand : 2 * operand + 2, t * P : (t + 1) * P, :]
-                    source = flipped.rearrange("p g u r -> p g r u")
-                    if operand == 0:
-                        nc.vector.tensor_copy(out=target, in_=source)
-                    else:
-                        nc.scalar.copy(out=target, in_=source)
+                words = raw[:, t, :].bitcast(F32)
+                bank = psum.tile([P, BLOCK], F32, tag="bank")
+                flipped = bank[:].rearrange("p (g u r) -> p g u r", g=2, u=2)
+                for g in range(2):
+                    for u in range(2):
+                        nc.tensor.transpose(flipped[:, g, u, :], words[:, 256 * g + u : 256 * (g + 1) : 2], identity[:])
+                target = grouped_words[:, 2 * operand : 2 * operand + 2, rows, :]
+                source = flipped.rearrange("p g u r -> p g r u")
+                if operand == 0:
+                    nc.vector.tensor_copy(out=target, in_=source)
+                else:
+                    nc.scalar.copy(out=target, in_=source)
             for s in range(PASSES):
                 nc.vector.quantize_mx(
-                    out=a_codes[:, s, :].bitcast(FP8X4),
-                    scales=a_planes[:, s, :],
-                    in_=grouped[:, s, :, :].rearrange("p r t -> p (r t)"),
+                    out=a_codes[:, s, rows].bitcast(FP8X4),
+                    scales=a_planes[:, s, rows],
+                    in_=grouped[:, s, rows, :].rearrange("p r k -> p (r k)"),
                 )
 
-        for first in range(GATE_I * HIDDEN, (GATE_F + 1) * HIDDEN, BLOCK):
-            repeated = psum.tile([P, BLOCK], F32, tag="bank")
-            nc.tensor.matmul(out=repeated[:], lhsT=ones[:], rhs=b_row[:, first : first + BLOCK], start=True, stop=True)
-            nc.scalar.copy(out=bias_rows[:, first : first + BLOCK], in_=repeated[:])
-        stood_up = psum.tile([P, BLOCK], F32, tag="bank")
-        stood_up_tiles = stood_up[:].rearrange("p (m n) -> p m n", n=SPREAD)
-        per_gate = HIDDEN // P
-        for slot, gate in enumerate((GATE_Z, GATE_O)):
-            for j in range(per_gate):
-                first = gate * HIDDEN + j * P
+        def repeat_on_partitions(gate):
+            repeated = keep.tile([P, HIDDEN], BF16, name="bias_rows%d" % gate)
+            for block in range(BLOCKS):
+                first = gate * HIDDEN + block * BLOCK
+                bank = psum.tile([P, BLOCK], F32, tag="bank")
+                nc.tensor.matmul(out=bank[:], lhsT=ones[:], rhs=b_row[:, first : first + BLOCK], start=True, stop=True)
+                nc.scalar.copy(out=repeated[:, block * BLOCK : (block + 1) * BLOCK], in_=bank[:])
+            return repeated
+
+        def stand_on_partitions(gate, factor):
+            stood = keep.tile([P, HIDDEN // P], F32, name="bias_cols%d" % gate)
+            bank = psum.tile([P, BLOCK], F32, tag="bank")
+            spread = bank[:].rearrange("p (m n) -> p m n", n=SPREAD)
+            for m in range(HIDDEN // P):
+                first = gate * HIDDEN + m * P
                 nc.tensor.matmul(
-                    out=stood_up_tiles[:, slot * per_gate + j, :],
-                    lhsT=b_row[:, first : first + P],
-                    rhs=ones[:, 0:SPREAD],
-                    start=True,
-                    stop=True,
+                    out=spread[:, m, :], lhsT=b_row[:, first : first + P], rhs=ones[:, 0:SPREAD], start=True, stop=True
                 )
-        nc.vector.tensor_copy(
-            out=bias_cols[:, GATE_Z * per_gate : (GATE_Z + 1) * per_gate], in_=stood_up_tiles[:, 0:per_gate, 0]
-        )
-        nc.vector.tensor_scalar_mul(
-            out=bias_cols[:, GATE_O * per_gate : (GATE_O + 1) * per_gate],
-            in0=stood_up_tiles[:, per_gate : 2 * per_gate, 0],
-            scalar1=0.5,
-        )
+            nc.vector.tensor_scalar_mul(out=stood[:], in0=spread[:, 0 : HIDDEN // P, 0], scalar1=factor)
+            return stood
 
-        gates = ctx.enter_context(tc.tile_pool(name="gates", bufs=ROW_TILES))
-        results = ctx.enter_context(tc.tile_pool(name="results", bufs=2 * ROW_TILES))
+        def gate_by_rows(gate, block, t, bias_rows, func, scale, name):
+            cols = slice(gate * HIDDEN + block * BLOCK, gate * HIDDEN + (block + 1) * BLOCK)
+            rows = slice(t * P, (t + 1) * P)
+            acc = psum.tile([P, BLOCK], F32, tag="bank")
+            for s in range(PASSES):
+                nc.tensor.matmul_mx(
+                    out=acc[:],
+                    lhsT=a_codes[:, s, rows].bitcast(FP8X4),
+                    lhsT_scale=a_planes[:, s, rows],
+                    rhs=w_codes[:, s, cols].bitcast(FP8X4),
+                    rhs_scale=w_planes[4 * s : P, cols],
+                    start=(s == 0),
+                    stop=(s == PASSES - 1),
+                )
+            value = gates.tile([P, BLOCK], F32, name=name)
+            nc.vector.tensor_tensor(
+                out=value[:], in0=acc[:], in1=bias_rows[:, block * BLOCK : (block + 1) * BLOCK], op=ALU.add
+            )
+            nc.scalar.activation(out=value[:], in_=value[:], func=func, scale=scale)
+            return value
 
-        def gate_by_rows(gate, block, func, scale, name):
-            first = gate * HIDDEN + block * BLOCK
-            cols = slice(first, first + BLOCK)
-            values = []
-            for t in tiles:
-                rows = slice(t * P, (t + 1) * P)
-                acc = psum.tile([P, BLOCK], F32, tag="bank")
-                for s in range(PASSES):
-                    nc.tensor.matmul_mx(
-                        out=acc[:],
-                        lhsT=a_codes[:, s, rows].bitcast(FP8X4),
-                        lhsT_scale=a_planes[:, s, rows],
-                        rhs=w_codes[:, s, cols].bitcast(FP8X4),
-                        rhs_scale=w_planes[4 * s : P, cols],
-                        start=(s == 0),
-                        stop=(s == PASSES - 1),
-                    )
-                value = gates.tile([P, BLOCK], F32, name=name)
-                nc.vector.tensor_tensor(out=value[:], in0=acc[:], in1=bias_rows[:, cols], op=ALU.add)
-                nc.scalar.activation(out=value[:], in_=value[:], func=func, scale=scale)
-                values.append(value)
-            return values
-
-        def gate_by_columns(gate, block, scale, name):
+        def gate_by_columns(gate, block, bias_cols, scale, name):
             values = []
             for j in range(COL_TILES):
-                first = gate * HIDDEN + block * BLOCK + j * P
-                cols = slice(first, first + P)
+                m = block * COL_TILES + j
+                cols = slice(gate * HIDDEN + m * P, gate * HIDDEN + (m + 1) * P)
                 acc = psum.tile([P, BATCH], F32, tag="bank")
                 for s in range(PASSES):
                     nc.tensor.matmul_mx(
@@ -185,9 +181,7 @@ def tile_slstmcell_kernel(
                         stop=(s == PASSES - 1),
                     )
                 value = gates.tile([P, BATCH], F32, name=name)
-                nc.scalar.activation(
-                    out=value[:], in_=acc[:], func=ACT.Tanh, bias=bias_cols[:, first // P : first // P + 1], scale=scale
-                )
+                nc.scalar.activation(out=value[:], in_=acc[:], func=ACT.Tanh, bias=bias_cols[:, m : m + 1], scale=scale)
                 values.append(value)
             return values
 
@@ -198,17 +192,19 @@ def tile_slstmcell_kernel(
                     nc.tensor.transpose(banks[t][:, j * P : (j + 1) * P], value[:, t * P : (t + 1) * P], identity[:])
             return banks
 
-        exp_i = gate_by_rows(GATE_I, 0, ACT.Exp, 1.0, "exp_i")
+        for t in tiles:
+            quantise_rows(t)
+        bias_f = repeat_on_partitions(GATE_F)
+        bias_i = repeat_on_partitions(GATE_I)
+        bias_z = stand_on_partitions(GATE_Z, 1.0)
+        half_bias_o = stand_on_partitions(GATE_O, 0.5)
+        tanh_f = [gate_by_rows(GATE_F, 0, t, bias_f, ACT.Tanh, 0.5, "tanh_f") for t in tiles]
+
         for block in range(BLOCKS):
             cols = slice(block * BLOCK, (block + 1) * BLOCK)
-            z_cols = gate_by_columns(GATE_Z, block, 1.0, "z_cols")
-            tanh_f = gate_by_rows(GATE_F, block, ACT.Tanh, 0.5, "tanh_f")
-            z = rows_onto_partitions(z_cols, "z")
-            tanh_o_cols = gate_by_columns(GATE_O, block, 0.5, "tanh_o_cols")
-            if block == 0:
-                nc.vector.tensor_scalar_mul(out=n_half[:], in0=n_old[:], scalar1=0.5)
-
-            c_new, n_new, h_new, iz, inverse = [], [], [], [], []
+            c_new, n_new, iz, inverse, half_ratio = [], [], [], [], []
+            nc.vector.tensor_scalar_mul(out=n_half[:, :, cols], in0=n_old[:, :, cols], scalar1=0.5)
+            exp_i = [gate_by_rows(GATE_I, block, t, bias_i, ACT.Exp, 1.0, "exp_i") for t in tiles]
             for t in tiles:
                 c_new.append(results.tile([P, BLOCK], F32, name="c_new"))
                 n_new.append(results.tile([P, BLOCK], F32, name="n_new"))
@@ -218,36 +214,38 @@ def tile_slstmcell_kernel(
                 nc.vector.scalar_tensor_tensor(
                     out=n_new[t][:], in0=tanh_f[t][:], scalar=1.0, in1=n_half[:, t, cols], op0=ALU.add, op1=ALU.mult
                 )
+            z = rows_onto_partitions(gate_by_columns(GATE_Z, block, bias_z, 1.0, "z_cols"), "z")
+            for t in tiles:
+                nc.vector.scalar_tensor_tensor(
+                    out=n_new[t][:], in0=exp_i[t][:], scalar=I_MAX, in1=n_new[t][:], op0=ALU.min, op1=ALU.add
+                )
+                nc.sync.dma_start(out=n_out[t * P : (t + 1) * P, cols], in_=n_new[t][:])
+                inverse.append(gates.tile([P, BLOCK], F32, name="inverse"))
+                nc.scalar.activation(out=inverse[t][:], in_=n_new[t][:], func=ACT.Ln, bias=eps[:])
             for t in tiles:
                 iz.append(gates.tile([P, BLOCK], F32, name="iz"))
                 nc.vector.scalar_tensor_tensor(
                     out=iz[t][:], in0=exp_i[t][:], scalar=I_MAX, in1=z[t][:], op0=ALU.min, op1=ALU.mult
                 )
             for t in tiles:
-                rows = slice(t * P, (t + 1) * P)
                 nc.vector.scalar_tensor_tensor(
                     out=c_new[t][:], in0=c_new[t][:], scalar=0.5, in1=iz[t][:], op0=ALU.mult, op1=ALU.add
                 )
-                nc.vector.scalar_tensor_tensor(
-                    out=n_new[t][:], in0=exp_i[t][:], scalar=I_MAX, in1=n_new[t][:], op0=ALU.min, op1=ALU.add
-                )
-                nc.sync.dma_start(out=c_out[rows, cols], in_=c_new[t][:])
-                nc.sync.dma_start(out=n_out[rows, cols], in_=n_new[t][:])
-                inverse.append(gates.tile([P, BLOCK], F32, name="inverse"))
-                nc.scalar.activation(out=inverse[t][:], in_=n_new[t][:], func=ACT.Ln, bias=eps[:])
+                nc.sync.dma_start(out=c_out[t * P : (t + 1) * P, cols], in_=c_new[t][:])
             for t in tiles:
                 nc.scalar.activation(out=inverse[t][:], in_=inverse[t][:], func=ACT.Exp, scale=-1.0)
+            tanh_o_cols = gate_by_columns(GATE_O, block, half_bias_o, 0.5, "tanh_o_cols")
             if block + 1 < BLOCKS:
-                exp_i = gate_by_rows(GATE_I, block + 1, ACT.Exp, 1.0, "exp_i")
+                tanh_f = [gate_by_rows(GATE_F, block + 1, t, bias_f, ACT.Tanh, 0.5, "tanh_f") for t in tiles]
             tanh_o = rows_onto_partitions(tanh_o_cols, "tanh_o")
             for t in tiles:
-                h_new.append(results.tile([P, BLOCK], F32, name="h_new"))
+                half_ratio.append(gates.tile([P, BLOCK], F32, name="half_ratio"))
                 nc.vector.scalar_tensor_tensor(
-                    out=h_new[t][:], in0=tanh_o[t][:], scalar=1.0, in1=c_new[t][:], op0=ALU.add, op1=ALU.mult
+                    out=half_ratio[t][:], in0=c_new[t][:], scalar=0.5, in1=inverse[t][:], op0=ALU.mult, op1=ALU.mult
                 )
             for t in tiles:
-                rows = slice(t * P, (t + 1) * P)
+                h_new = results.tile([P, BLOCK], F32, name="h_new")
                 nc.vector.scalar_tensor_tensor(
-                    out=h_new[t][:], in0=h_new[t][:], scalar=0.5, in1=inverse[t][:], op0=ALU.mult, op1=ALU.mult
+                    out=h_new[:], in0=tanh_o[t][:], scalar=1.0, in1=half_ratio[t][:], op0=ALU.add, op1=ALU.mult
                 )
-                nc.sync.dma_start(out=h_out[rows, cols], in_=h_new[t][:])
+                nc.sync.dma_start(out=h_out[t * P : (t + 1) * P, cols], in_=h_new[:])

@@ -49,7 +49,7 @@ def tile_slstmcell_kernel(
         n_old = keep.tile([P, ROW_TILES, HIDDEN], BF16)
         n_half = keep.tile([P, ROW_TILES, HIDDEN], BF16)
         identity = keep.tile([P, P], F32)
-        eps = keep.tile([P, 1], F32)
+        two_eps = keep.tile([P, 1], F32)
         b_row = stage.tile([P, 4 * HIDDEN], BF16)
         ones = stage.tile([P, P], BF16)
         x_raw = stage.tile([P, ROW_TILES, HIDDEN], BF16)
@@ -59,7 +59,7 @@ def tile_slstmcell_kernel(
         nc.vector.memset(w_planes[:].bitcast(I32), 0)
         nc.vector.memset(b_row[:].bitcast(I32), 0)
         nc.vector.memset(ones[:], 1.0)
-        nc.vector.memset(eps[:], EPS)
+        nc.vector.memset(two_eps[:], 2.0 * EPS)
         make_identity(nc, identity[:])
 
         def row_tiled(dram):
@@ -94,9 +94,12 @@ def tile_slstmcell_kernel(
         nc.sync.dma_start(out=b_row[0:1, :], in_=b.rearrange("(o n) -> o n", o=1))
         for block in range(BLOCKS):
             load_weight_block(GATE_F, block)
+            load_weight_block(GATE_Z, block)
             load_state_block(block)
-            for gate in (GATE_I, GATE_Z, GATE_O):
-                load_weight_block(gate, block)
+            if block > 0:
+                load_weight_block(GATE_O, block - 1)
+            load_weight_block(GATE_I, block)
+        load_weight_block(GATE_O, BLOCKS - 1)
 
         grouped_words = grouped[:].bitcast(F32)
 
@@ -198,30 +201,48 @@ def tile_slstmcell_kernel(
         bias_i = repeat_on_partitions(GATE_I)
         bias_z = stand_on_partitions(GATE_Z, 1.0)
         half_bias_o = stand_on_partitions(GATE_O, 0.5)
-        tanh_f = [gate_by_rows(GATE_F, 0, t, bias_f, ACT.Tanh, 0.5, "tanh_f") for t in tiles]
 
+        def f_gate(block):
+            return [gate_by_rows(GATE_F, block, t, bias_f, ACT.Tanh, 0.5, "tanh_f") for t in tiles]
+
+        def o_gate(block):
+            return gate_by_columns(GATE_O, block, half_bias_o, 0.5, "tanh_o_cols")
+
+        def finish_h(block, tanh_o_cols, half_ratio):
+            tanh_o = rows_onto_partitions(tanh_o_cols, "tanh_o")
+            for t in tiles:
+                h_new = results.tile([P, BLOCK], F32, name="h_new")
+                nc.vector.scalar_tensor_tensor(
+                    out=h_new[:], in0=tanh_o[t][:], scalar=1.0, in1=half_ratio[t][:], op0=ALU.add, op1=ALU.mult
+                )
+                nc.sync.dma_start(out=h_out[t * P : (t + 1) * P, block * BLOCK : (block + 1) * BLOCK], in_=h_new[:])
+
+        tanh_f = f_gate(0)
         for block in range(BLOCKS):
             cols = slice(block * BLOCK, (block + 1) * BLOCK)
-            c_new, n_new, iz, inverse, half_ratio = [], [], [], [], []
+            c_new, n_new, iz, inverse = [], [], [], []
+            z_cols = gate_by_columns(GATE_Z, block, bias_z, 1.0, "z_cols")
             nc.vector.tensor_scalar_mul(out=n_half[:, :, cols], in0=n_old[:, :, cols], scalar1=0.5)
-            exp_i = [gate_by_rows(GATE_I, block, t, bias_i, ACT.Exp, 1.0, "exp_i") for t in tiles]
             for t in tiles:
                 c_new.append(results.tile([P, BLOCK], F32, name="c_new"))
                 n_new.append(results.tile([P, BLOCK], F32, name="n_new"))
                 nc.vector.scalar_tensor_tensor(
-                    out=c_new[t][:], in0=tanh_f[t][:], scalar=1.0, in1=c_old[:, t, cols], op0=ALU.add, op1=ALU.mult
-                )
-                nc.vector.scalar_tensor_tensor(
                     out=n_new[t][:], in0=tanh_f[t][:], scalar=1.0, in1=n_half[:, t, cols], op0=ALU.add, op1=ALU.mult
                 )
-            z = rows_onto_partitions(gate_by_columns(GATE_Z, block, bias_z, 1.0, "z_cols"), "z")
+                nc.vector.scalar_tensor_tensor(
+                    out=c_new[t][:], in0=tanh_f[t][:], scalar=1.0, in1=c_old[:, t, cols], op0=ALU.add, op1=ALU.mult
+                )
+            if block > 0:
+                tanh_o_cols = o_gate(block - 1)
+            exp_i = [gate_by_rows(GATE_I, block, t, bias_i, ACT.Exp, 1.0, "exp_i") for t in tiles]
+            z = rows_onto_partitions(z_cols, "z")
             for t in tiles:
                 nc.vector.scalar_tensor_tensor(
                     out=n_new[t][:], in0=exp_i[t][:], scalar=I_MAX, in1=n_new[t][:], op0=ALU.min, op1=ALU.add
                 )
                 nc.sync.dma_start(out=n_out[t * P : (t + 1) * P, cols], in_=n_new[t][:])
                 inverse.append(gates.tile([P, BLOCK], F32, name="inverse"))
-                nc.scalar.activation(out=inverse[t][:], in_=n_new[t][:], func=ACT.Ln, bias=eps[:])
+                nc.scalar.activation(out=inverse[t][:], in_=n_new[t][:], func=ACT.Ln, bias=two_eps[:], scale=2.0)
             for t in tiles:
                 iz.append(gates.tile([P, BLOCK], F32, name="iz"))
                 nc.vector.scalar_tensor_tensor(
@@ -234,18 +255,12 @@ def tile_slstmcell_kernel(
                 nc.sync.dma_start(out=c_out[t * P : (t + 1) * P, cols], in_=c_new[t][:])
             for t in tiles:
                 nc.scalar.activation(out=inverse[t][:], in_=inverse[t][:], func=ACT.Exp, scale=-1.0)
-            tanh_o_cols = gate_by_columns(GATE_O, block, half_bias_o, 0.5, "tanh_o_cols")
+            if block > 0:
+                finish_h(block - 1, tanh_o_cols, half_ratio)
             if block + 1 < BLOCKS:
-                tanh_f = [gate_by_rows(GATE_F, block + 1, t, bias_f, ACT.Tanh, 0.5, "tanh_f") for t in tiles]
-            tanh_o = rows_onto_partitions(tanh_o_cols, "tanh_o")
+                tanh_f = f_gate(block + 1)
+            half_ratio = []
             for t in tiles:
                 half_ratio.append(gates.tile([P, BLOCK], F32, name="half_ratio"))
-                nc.vector.scalar_tensor_tensor(
-                    out=half_ratio[t][:], in0=c_new[t][:], scalar=0.5, in1=inverse[t][:], op0=ALU.mult, op1=ALU.mult
-                )
-            for t in tiles:
-                h_new = results.tile([P, BLOCK], F32, name="h_new")
-                nc.vector.scalar_tensor_tensor(
-                    out=h_new[:], in0=tanh_o[t][:], scalar=1.0, in1=half_ratio[t][:], op0=ALU.add, op1=ALU.mult
-                )
-                nc.sync.dma_start(out=h_out[t * P : (t + 1) * P, cols], in_=h_new[:])
+                nc.vector.tensor_tensor(out=half_ratio[t][:], in0=c_new[t][:], in1=inverse[t][:], op=ALU.mult)
+        finish_h(BLOCKS - 1, o_gate(BLOCKS - 1), half_ratio)

@@ -13,19 +13,29 @@ ACT = mybir.ActivationFunctionType
 ALU = mybir.AluOpType
 
 P = 128
+PSUM_BANKS = 8
 BATCH = 512
 HIDDEN = 1024
-PASSES = 4
+GATES = 4
+GATE_Z, GATE_I, GATE_F, GATE_O = 0, 1, 2, 3
+PACK = 4
+K_PASS = P * PACK
+OPERAND_PASSES = HIDDEN // K_PASS
+PASSES = 2 * OPERAND_PASSES
+PAIRS = PACK // 2
+PASS_WORDS = K_PASS // 2
+QUADRANT = 32
+QUADRANTS = P // QUADRANT
+PLANE_ROWS = 4
 ROW_TILES = BATCH // P
 BLOCK = 512
 BLOCKS = HIDDEN // BLOCK
 COL_TILES = BLOCK // P
-GATE_Z, GATE_I, GATE_F, GATE_O = 0, 1, 2, 3
 EPS = 1e-6
 I_MAX = 50.0
 SPREAD = 32
 
-FLOPS = 2 * BATCH * (2 * HIDDEN) * (4 * HIDDEN)
+FLOPS = 2 * BATCH * (2 * HIDDEN) * (GATES * HIDDEN)
 
 
 def tile_slstmcell_kernel(
@@ -36,118 +46,129 @@ def tile_slstmcell_kernel(
     with ExitStack() as ctx:
         ctx.enter_context(tc.manual_schedule())
         keep = ctx.enter_context(tc.tile_pool(name="keep", bufs=1))
-        psum = ctx.enter_context(tc.psum_pool(name="psum", bufs=8))
+        psum = ctx.enter_context(tc.psum_pool(name="psum", bufs=PSUM_BANKS))
         gates = ctx.enter_context(tc.tile_pool(name="gates", bufs=ROW_TILES))
-        results = ctx.enter_context(tc.tile_pool(name="results", bufs=ROW_TILES))
-        stage = ctx.enter_context(tc.tile_pool(name="stage", bufs=1))
 
-        w_codes = keep.tile([P, PASSES, 4 * HIDDEN], U32, align_bytes=64)
+        w_codes = keep.tile([P, PASSES, GATES * HIDDEN], U32, align_bytes=64)
         a_codes = keep.tile([P, PASSES, BATCH], U32, align_bytes=64)
-        w_planes = keep.tile([P, 4 * HIDDEN], U8, align_bytes=64)
+        w_planes = keep.tile([P, GATES * HIDDEN], U8, align_bytes=64)
         a_planes = keep.tile([P, PASSES, BATCH], U8, align_bytes=64)
         c_old = keep.tile([P, ROW_TILES, HIDDEN], BF16)
         n_old = keep.tile([P, ROW_TILES, HIDDEN], BF16)
         n_half = keep.tile([P, ROW_TILES, HIDDEN], BF16)
         identity = keep.tile([P, P], F32)
         two_eps = keep.tile([P, 1], F32)
-        b_row = stage.tile([P, 4 * HIDDEN], BF16)
-        ones = stage.tile([P, P], BF16)
-        x_raw = stage.tile([P, ROW_TILES, HIDDEN], BF16)
-        h_raw = stage.tile([P, ROW_TILES, HIDDEN], BF16)
-        grouped = stage.tile([P, PASSES, BATCH, 4], BF16, align_bytes=64)
-
-        nc.vector.memset(w_planes[:].bitcast(I32), 0)
-        nc.vector.memset(b_row[:].bitcast(I32), 0)
-        nc.vector.memset(ones[:], 1.0)
-        nc.vector.memset(two_eps[:], 2.0 * EPS)
-        make_identity(nc, identity[:])
 
         def row_tiled(dram):
-            return dram.rearrange("(t p) d -> p t d", p=P)
+            return dram.rearrange("(p t) d -> p t d", t=ROW_TILES)
 
-        def load_rows(t):
-            nc.sync.dma_start(out=x_raw[:, t, :], in_=row_tiled(x_t)[:, t, :])
-            nc.sync.dma_start(out=h_raw[:, t, :], in_=row_tiled(h_prev)[:, t, :])
+        def load_and_prepare(stage):
+            b_row = stage.tile([P, GATES * HIDDEN], BF16)
+            ones = stage.tile([P, P], BF16)
+            x_raw = stage.tile([P, ROW_TILES, HIDDEN], BF16)
+            h_raw = stage.tile([P, ROW_TILES, HIDDEN], BF16)
+            grouped = stage.tile([P, PASSES, BATCH, PACK], BF16, align_bytes=64)
 
-        def load_weight_block(gate, block):
-            first = gate * HIDDEN + block * BLOCK
-            for operand, words in enumerate((W_words, R_words)):
-                nc.sync.dma_start(
-                    out=w_codes[:, 2 * operand : 2 * operand + 2, first : first + BLOCK].bitcast(I32),
-                    in_=words.rearrange("g p n t -> p g (n t)")[:, :, 4 * first : 4 * (first + BLOCK)].bitcast(I32),
-                )
+            nc.vector.memset(w_planes[:].bitcast(I32), 0)
+            nc.vector.memset(b_row[:].bitcast(I32), 0)
+            nc.vector.memset(ones[:], 1.0)
+            nc.vector.memset(two_eps[:], 2.0 * EPS)
+            make_identity(nc, identity[:])
 
-        def load_state_block(block):
-            cols = slice(block * BLOCK, (block + 1) * BLOCK)
-            nc.sync.dma_start(out=n_old[:, :, cols], in_=row_tiled(n_prev)[:, :, cols])
-            nc.sync.dma_start(out=c_old[:, :, cols], in_=row_tiled(c_prev)[:, :, cols])
-
-        for t in tiles:
-            load_rows(t)
-        for quadrant in range(4):
-            for operand, scales in enumerate((W_scales, R_scales)):
-                first = 32 * quadrant + 8 * operand
-                nc.sync.dma_start(
-                    out=w_planes[first : first + 8, :].bitcast(I32),
-                    in_=scales[:, 4 * quadrant : 4 * quadrant + 4, :].bitcast(I32),
-                )
-        nc.sync.dma_start(out=b_row[0:1, :], in_=b.rearrange("(o n) -> o n", o=1))
-        for block in range(BLOCKS):
-            load_weight_block(GATE_F, block)
-            load_weight_block(GATE_Z, block)
-            load_state_block(block)
-            if block > 0:
-                load_weight_block(GATE_O, block - 1)
-            load_weight_block(GATE_I, block)
-        load_weight_block(GATE_O, BLOCKS - 1)
-
-        grouped_words = grouped[:].bitcast(F32)
-
-        def quantise_rows(t):
-            rows = slice(t * P, (t + 1) * P)
-            for operand, raw in enumerate((x_raw, h_raw)):
-                words = raw[:, t, :].bitcast(F32)
-                bank = psum.tile([P, BLOCK], F32, tag="bank")
-                flipped = bank[:].rearrange("p (g u r) -> p g u r", g=2, u=2)
-                for g in range(2):
-                    for u in range(2):
-                        nc.tensor.transpose(flipped[:, g, u, :], words[:, 256 * g + u : 256 * (g + 1) : 2], identity[:])
-                target = grouped_words[:, 2 * operand : 2 * operand + 2, rows, :]
-                source = flipped.rearrange("p g u r -> p g r u")
-                if operand == 0:
-                    nc.vector.tensor_copy(out=target, in_=source)
-                else:
-                    nc.scalar.copy(out=target, in_=source)
-            for s in range(PASSES):
-                nc.vector.quantize_mx(
-                    out=a_codes[:, s, rows].bitcast(FP8X4),
-                    scales=a_planes[:, s, rows],
-                    in_=grouped[:, s, rows, :].rearrange("p r k -> p (r k)"),
-                )
-
-        def repeat_on_partitions(gate):
-            repeated = keep.tile([P, HIDDEN], BF16, name="bias_rows%d" % gate)
-            for block in range(BLOCKS):
+            def load_weight_block(gate, block):
                 first = gate * HIDDEN + block * BLOCK
-                bank = psum.tile([P, BLOCK], F32, tag="bank")
-                nc.tensor.matmul(out=bank[:], lhsT=ones[:], rhs=b_row[:, first : first + BLOCK], start=True, stop=True)
-                nc.scalar.copy(out=repeated[:, block * BLOCK : (block + 1) * BLOCK], in_=bank[:])
-            return repeated
+                for operand, words in enumerate((W_words, R_words)):
+                    passes = slice(OPERAND_PASSES * operand, OPERAND_PASSES * (operand + 1))
+                    nc.sync.dma_start(
+                        out=w_codes[:, passes, first : first + BLOCK].bitcast(I32),
+                        in_=words.rearrange("g p n t -> p g (n t)")[:, :, PACK * first : PACK * (first + BLOCK)].bitcast(I32),
+                    )
 
-        def stand_on_partitions(gate, factor):
-            stood = keep.tile([P, HIDDEN // P], F32, name="bias_cols%d" % gate)
-            bank = psum.tile([P, BLOCK], F32, tag="bank")
-            spread = bank[:].rearrange("p (m n) -> p m n", n=SPREAD)
-            for m in range(HIDDEN // P):
-                first = gate * HIDDEN + m * P
-                nc.tensor.matmul(
-                    out=spread[:, m, :], lhsT=b_row[:, first : first + P], rhs=ones[:, 0:SPREAD], start=True, stop=True
-                )
-            nc.vector.tensor_scalar_mul(out=stood[:], in0=spread[:, 0 : HIDDEN // P, 0], scalar1=factor)
-            return stood
+            def load_state_block(block):
+                cols = slice(block * BLOCK, (block + 1) * BLOCK)
+                nc.sync.dma_start(out=n_old[:, :, cols], in_=row_tiled(n_prev)[:, :, cols])
+                nc.sync.dma_start(out=c_old[:, :, cols], in_=row_tiled(c_prev)[:, :, cols])
+
+            nc.sync.dma_start(out=x_raw[:], in_=row_tiled(x_t))
+            nc.sync.dma_start(out=h_raw[:], in_=row_tiled(h_prev))
+            for quadrant in range(QUADRANTS):
+                for operand, scales in enumerate((W_scales, R_scales)):
+                    top = QUADRANT * quadrant + OPERAND_PASSES * PLANE_ROWS * operand
+                    nc.sync.dma_start(
+                        out=w_planes[top : top + OPERAND_PASSES * PLANE_ROWS, :].bitcast(I32),
+                        in_=scales[:, PLANE_ROWS * quadrant : PLANE_ROWS * (quadrant + 1), :].bitcast(I32),
+                    )
+            nc.sync.dma_start(out=b_row[0:1, :], in_=b.rearrange("(o n) -> o n", o=1))
+            for block in range(BLOCKS):
+                load_weight_block(GATE_F, block)
+                load_weight_block(GATE_Z, block)
+                load_state_block(block)
+                if block > 0:
+                    load_weight_block(GATE_O, block - 1)
+                load_weight_block(GATE_I, block)
+            load_weight_block(GATE_O, BLOCKS - 1)
+
+            grouped_words = grouped[:].bitcast(F32)
+
+            def quantise_rows(t):
+                rows = slice(t * P, (t + 1) * P)
+                for operand, raw in enumerate((x_raw, h_raw)):
+                    words = raw[:, t, :].bitcast(F32)
+                    bank = psum.tile([P, BLOCK], F32, tag="bank")
+                    flipped = bank[:].rearrange("p (g u r) -> p g u r", g=OPERAND_PASSES, u=PAIRS)
+                    for g in range(OPERAND_PASSES):
+                        for u in range(PAIRS):
+                            nc.tensor.transpose(
+                                flipped[:, g, u, :], words[:, PASS_WORDS * g + u : PASS_WORDS * (g + 1) : PAIRS], identity[:]
+                            )
+                    target = grouped_words[:, OPERAND_PASSES * operand : OPERAND_PASSES * (operand + 1), rows, :]
+                    source = flipped.rearrange("p g u r -> p g r u")
+                    if operand == 0:
+                        nc.vector.tensor_copy(out=target, in_=source)
+                    else:
+                        nc.scalar.copy(out=target, in_=source)
+                for s in range(PASSES):
+                    nc.vector.quantize_mx(
+                        out=a_codes[:, s, rows].bitcast(FP8X4),
+                        scales=a_planes[:, s, rows],
+                        in_=grouped[:, s, rows, :].rearrange("p r k -> p (r k)"),
+                    )
+
+            def repeat_on_partitions(gate):
+                repeated = keep.tile([P, HIDDEN], BF16, name="bias_rows%d" % gate)
+                for block in range(BLOCKS):
+                    first = gate * HIDDEN + block * BLOCK
+                    bank = psum.tile([P, BLOCK], F32, tag="bank")
+                    nc.tensor.matmul(out=bank[:], lhsT=ones[:], rhs=b_row[:, first : first + BLOCK], start=True, stop=True)
+                    nc.scalar.copy(out=repeated[:, block * BLOCK : (block + 1) * BLOCK], in_=bank[:])
+                return repeated
+
+            def stand_on_partitions(gate, factor):
+                stood = keep.tile([P, HIDDEN // P], F32, name="bias_cols%d" % gate)
+                bank = psum.tile([P, BLOCK], F32, tag="bank")
+                spread = bank[:].rearrange("p (m n) -> p m n", n=SPREAD)
+                for m in range(HIDDEN // P):
+                    first = gate * HIDDEN + m * P
+                    nc.tensor.matmul(
+                        out=spread[:, m, :], lhsT=b_row[:, first : first + P], rhs=ones[:, 0:SPREAD], start=True, stop=True
+                    )
+                nc.vector.tensor_scalar_mul(out=stood[:], in0=spread[:, 0 : HIDDEN // P, 0], scalar1=factor)
+                return stood
+
+            for t in tiles:
+                quantise_rows(t)
+            bias_f = repeat_on_partitions(GATE_F)
+            bias_i = repeat_on_partitions(GATE_I)
+            bias_z = stand_on_partitions(GATE_Z, 1.0)
+            half_bias_o = stand_on_partitions(GATE_O, 0.5)
+            return bias_f, bias_i, bias_z, half_bias_o
+
+        with tc.tile_pool(name="stage", bufs=1) as stage:
+            bias_f, bias_i, bias_z, half_bias_o = load_and_prepare(stage)
+        results = ctx.enter_context(tc.tile_pool(name="results", bufs=BLOCKS * ROW_TILES))
 
         def gate_by_rows(gate, block, t, bias_rows, func, scale, name):
-            cols = slice(gate * HIDDEN + block * BLOCK, gate * HIDDEN + (block + 1) * BLOCK)
+            pre_cols = slice(gate * HIDDEN + block * BLOCK, gate * HIDDEN + (block + 1) * BLOCK)
             rows = slice(t * P, (t + 1) * P)
             acc = psum.tile([P, BLOCK], F32, tag="bank")
             for s in range(PASSES):
@@ -155,8 +176,8 @@ def tile_slstmcell_kernel(
                     out=acc[:],
                     lhsT=a_codes[:, s, rows].bitcast(FP8X4),
                     lhsT_scale=a_planes[:, s, rows],
-                    rhs=w_codes[:, s, cols].bitcast(FP8X4),
-                    rhs_scale=w_planes[4 * s : P, cols],
+                    rhs=w_codes[:, s, pre_cols].bitcast(FP8X4),
+                    rhs_scale=w_planes[PLANE_ROWS * s : P, pre_cols],
                     start=(s == 0),
                     stop=(s == PASSES - 1),
                 )
@@ -171,13 +192,13 @@ def tile_slstmcell_kernel(
             values = []
             for j in range(COL_TILES):
                 m = block * COL_TILES + j
-                cols = slice(gate * HIDDEN + m * P, gate * HIDDEN + (m + 1) * P)
+                pre_cols = slice(gate * HIDDEN + m * P, gate * HIDDEN + (m + 1) * P)
                 acc = psum.tile([P, BATCH], F32, tag="bank")
                 for s in range(PASSES):
                     nc.tensor.matmul_mx(
                         out=acc[:],
-                        lhsT=w_codes[:, s, cols].bitcast(FP8X4),
-                        lhsT_scale=w_planes[4 * s : P, cols],
+                        lhsT=w_codes[:, s, pre_cols].bitcast(FP8X4),
+                        lhsT_scale=w_planes[PLANE_ROWS * s : P, pre_cols],
                         rhs=a_codes[:, s, :].bitcast(FP8X4),
                         rhs_scale=a_planes[:, s, :],
                         start=(s == 0),
@@ -195,13 +216,6 @@ def tile_slstmcell_kernel(
                     nc.tensor.transpose(banks[t][:, j * P : (j + 1) * P], value[:, t * P : (t + 1) * P], identity[:])
             return banks
 
-        for t in tiles:
-            quantise_rows(t)
-        bias_f = repeat_on_partitions(GATE_F)
-        bias_i = repeat_on_partitions(GATE_I)
-        bias_z = stand_on_partitions(GATE_Z, 1.0)
-        half_bias_o = stand_on_partitions(GATE_O, 0.5)
-
         def f_gate(block):
             return [gate_by_rows(GATE_F, block, t, bias_f, ACT.Tanh, 0.5, "tanh_f") for t in tiles]
 
@@ -215,7 +229,7 @@ def tile_slstmcell_kernel(
                 nc.vector.scalar_tensor_tensor(
                     out=h_new[:], in0=tanh_o[t][:], scalar=1.0, in1=half_ratio[t][:], op0=ALU.add, op1=ALU.mult
                 )
-                nc.sync.dma_start(out=h_out[t * P : (t + 1) * P, block * BLOCK : (block + 1) * BLOCK], in_=h_new[:])
+                nc.sync.dma_start(out=row_tiled(h_out)[:, t, block * BLOCK : (block + 1) * BLOCK], in_=h_new[:])
 
         tanh_f = f_gate(0)
         for block in range(BLOCKS):
@@ -240,7 +254,7 @@ def tile_slstmcell_kernel(
                 nc.vector.scalar_tensor_tensor(
                     out=n_new[t][:], in0=exp_i[t][:], scalar=I_MAX, in1=n_new[t][:], op0=ALU.min, op1=ALU.add
                 )
-                nc.sync.dma_start(out=n_out[t * P : (t + 1) * P, cols], in_=n_new[t][:])
+                nc.sync.dma_start(out=row_tiled(n_out)[:, t, cols], in_=n_new[t][:])
                 inverse.append(gates.tile([P, BLOCK], F32, name="inverse"))
                 nc.scalar.activation(out=inverse[t][:], in_=n_new[t][:], func=ACT.Ln, bias=two_eps[:], scale=2.0)
             for t in tiles:
@@ -252,7 +266,7 @@ def tile_slstmcell_kernel(
                 nc.vector.scalar_tensor_tensor(
                     out=c_new[t][:], in0=c_new[t][:], scalar=0.5, in1=iz[t][:], op0=ALU.mult, op1=ALU.add
                 )
-                nc.sync.dma_start(out=c_out[t * P : (t + 1) * P, cols], in_=c_new[t][:])
+                nc.sync.dma_start(out=row_tiled(c_out)[:, t, cols], in_=c_new[t][:])
             for t in tiles:
                 nc.scalar.activation(out=inverse[t][:], in_=inverse[t][:], func=ACT.Exp, scale=-1.0)
             if block > 0:

@@ -33,6 +33,7 @@ BLOCKS = HIDDEN // BLOCK
 COL_TILES = BLOCK // P
 EPS = 1e-6
 I_MAX = 50.0
+ON_GPSIMD = 2
 SPREAD = 32
 
 FLOPS = 2 * BATCH * (2 * HIDDEN) * (GATES * HIDDEN)
@@ -273,8 +274,8 @@ def tile_slstmcell_kernel(
                 finish_h(block - 1, tanh_o_cols, half_ratio)
             if block + 1 < BLOCKS:
                 tanh_f = f_gate(block + 1)
-            half_ratio = []
+            half_ratio = [gates.tile([P, BLOCK], F32, name="half_ratio") for t in tiles]
             for t in tiles:
-                half_ratio.append(gates.tile([P, BLOCK], F32, name="half_ratio"))
-                nc.vector.tensor_tensor(out=half_ratio[t][:], in0=c_new[t][:], in1=inverse[t][:], op=ALU.mult)
+                engine = nc.gpsimd if t >= ROW_TILES - ON_GPSIMD else nc.vector
+                engine.tensor_tensor(out=half_ratio[t][:], in0=c_new[t][:], in1=inverse[t][:], op=ALU.mult)
         finish_h(BLOCKS - 1, o_gate(BLOCKS - 1), half_ratio)

@@ -92,16 +92,22 @@ def tile_slstmcell_kernel(
 
             nc.sync.dma_start(out=x_raw[:], in_=row_tiled(x_t))
             nc.sync.dma_start(out=h_raw[:], in_=row_tiled(h_prev))
-            for quadrant in range(QUADRANTS):
-                for operand, scales in enumerate((W_scales, R_scales)):
-                    top = QUADRANT * quadrant + OPERAND_PASSES * PLANE_ROWS * operand
-                    nc.sync.dma_start(
-                        out=w_planes[top : top + OPERAND_PASSES * PLANE_ROWS, :].bitcast(I32),
-                        in_=scales[:, PLANE_ROWS * quadrant : PLANE_ROWS * (quadrant + 1), :].bitcast(I32),
-                    )
+            def load_scales(first_gate, last_gate):
+                cols = slice(first_gate * HIDDEN, (last_gate + 1) * HIDDEN)
+                for quadrant in range(QUADRANTS):
+                    for operand, scales in enumerate((W_scales, R_scales)):
+                        top = QUADRANT * quadrant + OPERAND_PASSES * PLANE_ROWS * operand
+                        nc.sync.dma_start(
+                            out=w_planes[top : top + OPERAND_PASSES * PLANE_ROWS, cols].bitcast(I32),
+                            in_=scales[:, PLANE_ROWS * quadrant : PLANE_ROWS * (quadrant + 1), cols].bitcast(I32),
+                        )
+
+            load_scales(GATE_F, GATE_O)
             nc.sync.dma_start(out=b_row[0:1, :], in_=b.rearrange("(o n) -> o n", o=1))
             for block in range(BLOCKS):
                 load_weight_block(GATE_F, block)
+                if block == 0:
+                    load_scales(GATE_Z, GATE_I)
                 load_weight_block(GATE_Z, block)
                 load_state_block(block)
                 if block > 0:

@@ -102,7 +102,7 @@ def tile_slstmcell_kernel(
                             in_=scales[:, PLANE_ROWS * quadrant : PLANE_ROWS * (quadrant + 1), cols].bitcast(I32),
                         )
 
-            load_scales(GATE_F, GATE_O)
+            load_scales(GATE_F, GATE_F)
             nc.sync.dma_start(out=b_row[0:1, :], in_=b.rearrange("(o n) -> o n", o=1))
             for block in range(BLOCKS):
                 load_weight_block(GATE_F, block)
@@ -111,6 +111,7 @@ def tile_slstmcell_kernel(
                 load_weight_block(GATE_Z, block)
                 load_state_block(block)
                 if block > 0:
+                    load_scales(GATE_O, GATE_O)
                     load_weight_block(GATE_O, block - 1)
                 load_weight_block(GATE_I, block)
             load_weight_block(GATE_O, BLOCKS - 1)

@@ -34,7 +34,6 @@ COL_TILES = BLOCK // P
 EPS = 1e-6
 I_MAX = 50.0
 ON_GPSIMD = 2
-SPREAD = 32
 
 FLOPS = 2 * BATCH * (2 * HIDDEN) * (GATES * HIDDEN)
 
@@ -52,7 +51,7 @@ def tile_slstmcell_kernel(
 
         w_codes = keep.tile([P, PASSES, GATES * HIDDEN], U32, align_bytes=64)
         a_codes = keep.tile([P, PASSES, BATCH], U32, align_bytes=64)
-        w_planes = keep.tile([P, GATES * HIDDEN], U8, align_bytes=64)
+        w_planes = [keep.tile([P, GATES * HIDDEN], U8, align_bytes=64, name="planes%d" % operand) for operand in range(2)]
         a_planes = keep.tile([P, PASSES, BATCH], U8, align_bytes=64)
         c_old = keep.tile([P, ROW_TILES, HIDDEN], BF16)
         n_old = keep.tile([P, ROW_TILES, HIDDEN], BF16)
@@ -64,225 +63,325 @@ def tile_slstmcell_kernel(
             return dram.rearrange("(p t) d -> p t d", t=ROW_TILES)
 
         def load_and_prepare(stage):
-            b_row = stage.tile([P, GATES * HIDDEN], BF16)
-            ones = stage.tile([P, P], BF16)
+            b_lines = stage.tile([P, P], BF16)
+            identity_bf = stage.tile([P, P], BF16)
             x_raw = stage.tile([P, ROW_TILES, HIDDEN], BF16)
             h_raw = stage.tile([P, ROW_TILES, HIDDEN], BF16)
-            grouped = stage.tile([P, PASSES, BATCH, PACK], BF16, align_bytes=64)
 
-            nc.vector.memset(w_planes[:].bitcast(I32), 0)
-            nc.vector.memset(b_row[:].bitcast(I32), 0)
-            nc.vector.memset(ones[:], 1.0)
-            nc.vector.memset(two_eps[:], 2.0 * EPS)
+            nc.gpsimd.memset(b_lines[:].bitcast(I32), 0)
+            nc.sync.dma_start(out=b_lines[0 : GATES * HIDDEN // P, :], in_=b.rearrange("(m p) -> m p", p=P))
             make_identity(nc, identity[:])
+            nc.vector.tensor_copy(out=identity_bf[:], in_=identity[:])
+            nc.vector.memset(w_planes[0][:].bitcast(I32), 0)
+            nc.gpsimd.memset(w_planes[1][:].bitcast(I32), 0)
+            nc.vector.memset(two_eps[:], 2.0 * EPS)
+
+            def load_weights(operand, gate, block):
+                first = gate * HIDDEN + block * BLOCK
+                passes = slice(OPERAND_PASSES * operand, OPERAND_PASSES * (operand + 1))
+                words = (W_words, R_words)[operand]
+                nc.sync.dma_start(
+                    out=w_codes[:, passes, first : first + BLOCK].bitcast(I32),
+                    in_=words.rearrange("g p n t -> p g (n t)")[:, :, PACK * first : PACK * (first + BLOCK)].bitcast(I32),
+                )
 
             def load_weight_block(gate, block):
-                first = gate * HIDDEN + block * BLOCK
-                for operand, words in enumerate((W_words, R_words)):
-                    passes = slice(OPERAND_PASSES * operand, OPERAND_PASSES * (operand + 1))
-                    nc.sync.dma_start(
-                        out=w_codes[:, passes, first : first + BLOCK].bitcast(I32),
-                        in_=words.rearrange("g p n t -> p g (n t)")[:, :, PACK * first : PACK * (first + BLOCK)].bitcast(I32),
-                    )
+                for operand in range(2):
+                    load_weights(operand, gate, block)
 
             def load_state_block(block):
                 cols = slice(block * BLOCK, (block + 1) * BLOCK)
                 nc.sync.dma_start(out=n_old[:, :, cols], in_=row_tiled(n_prev)[:, :, cols])
                 nc.sync.dma_start(out=c_old[:, :, cols], in_=row_tiled(c_prev)[:, :, cols])
 
-            nc.sync.dma_start(out=x_raw[:], in_=row_tiled(x_t))
-            nc.sync.dma_start(out=h_raw[:], in_=row_tiled(h_prev))
-            def load_scales(first_gate, last_gate):
+            def load_scales(operand, first_gate, last_gate):
                 cols = slice(first_gate * HIDDEN, (last_gate + 1) * HIDDEN)
+                scales = (W_scales, R_scales)[operand]
                 for quadrant in range(QUADRANTS):
-                    for operand, scales in enumerate((W_scales, R_scales)):
-                        top = QUADRANT * quadrant + OPERAND_PASSES * PLANE_ROWS * operand
-                        nc.sync.dma_start(
-                            out=w_planes[top : top + OPERAND_PASSES * PLANE_ROWS, cols].bitcast(I32),
-                            in_=scales[:, PLANE_ROWS * quadrant : PLANE_ROWS * (quadrant + 1), cols].bitcast(I32),
-                        )
-
-            load_scales(GATE_F, GATE_F)
-            nc.sync.dma_start(out=b_row[0:1, :], in_=b.rearrange("(o n) -> o n", o=1))
-            for block in range(BLOCKS):
-                load_weight_block(GATE_F, block)
-                if block == 0:
-                    load_scales(GATE_Z, GATE_I)
-                load_weight_block(GATE_Z, block)
-                load_state_block(block)
-                if block > 0:
-                    load_scales(GATE_O, GATE_O)
-                    load_weight_block(GATE_O, block - 1)
-                load_weight_block(GATE_I, block)
-            load_weight_block(GATE_O, BLOCKS - 1)
-
-            grouped_words = grouped[:].bitcast(F32)
-
-            def quantise_rows(t):
-                rows = slice(t * P, (t + 1) * P)
-                for operand, raw in enumerate((x_raw, h_raw)):
-                    words = raw[:, t, :].bitcast(F32)
-                    bank = psum.tile([P, BLOCK], F32, tag="bank")
-                    flipped = bank[:].rearrange("p (g u r) -> p g u r", g=OPERAND_PASSES, u=PAIRS)
-                    for g in range(OPERAND_PASSES):
-                        for u in range(PAIRS):
-                            nc.tensor.transpose(
-                                flipped[:, g, u, :], words[:, PASS_WORDS * g + u : PASS_WORDS * (g + 1) : PAIRS], identity[:]
-                            )
-                    target = grouped_words[:, OPERAND_PASSES * operand : OPERAND_PASSES * (operand + 1), rows, :]
-                    source = flipped.rearrange("p g u r -> p g r u")
-                    if operand == 0:
-                        nc.vector.tensor_copy(out=target, in_=source)
-                    else:
-                        nc.scalar.copy(out=target, in_=source)
-                for s in range(PASSES):
-                    nc.vector.quantize_mx(
-                        out=a_codes[:, s, rows].bitcast(FP8X4),
-                        scales=a_planes[:, s, rows],
-                        in_=grouped[:, s, rows, :].rearrange("p r k -> p (r k)"),
+                    top = QUADRANT * quadrant
+                    nc.sync.dma_start(
+                        out=w_planes[operand][top : top + OPERAND_PASSES * PLANE_ROWS, cols].bitcast(I32),
+                        in_=scales[:, PLANE_ROWS * quadrant : PLANE_ROWS * (quadrant + 1), cols].bitcast(I32),
                     )
+
+            nc.sync.dma_start(out=x_raw[:], in_=row_tiled(x_t))
+            load_scales(0, GATE_F, GATE_F)
+            load_weights(0, GATE_F, 0)
+            nc.sync.dma_start(out=h_raw[:], in_=row_tiled(h_prev))
+            load_scales(1, GATE_F, GATE_F)
+            load_weights(1, GATE_F, 0)
+            def load_both_scales(gate):
+                for operand in range(2):
+                    load_scales(operand, gate, gate)
+
+            load_both_scales(GATE_I)
+            load_weight_block(GATE_I, 0)
+            load_state_block(0)
+            load_both_scales(GATE_Z)
+            load_weight_block(GATE_Z, 0)
+            load_weight_block(GATE_F, 1)
+            load_state_block(1)
+            load_weight_block(GATE_I, 1)
+            load_weight_block(GATE_Z, 1)
+            load_both_scales(GATE_O)
+            for block in range(BLOCKS):
+                load_weight_block(GATE_O, block)
 
             def repeat_on_partitions(gate):
                 repeated = keep.tile([P, HIDDEN], BF16, name="bias_rows%d" % gate)
                 for block in range(BLOCKS):
-                    first = gate * HIDDEN + block * BLOCK
                     bank = psum.tile([P, BLOCK], F32, tag="bank")
-                    nc.tensor.matmul(out=bank[:], lhsT=ones[:], rhs=b_row[:, first : first + BLOCK], start=True, stop=True)
+                    for j in range(COL_TILES):
+                        m = (gate * HIDDEN + block * BLOCK) // P + j
+                        nc.tensor.matmul(
+                            out=bank[:, j * P : (j + 1) * P],
+                            lhsT=identity_bf[:, m : m + 1].to_broadcast([P, P]),
+                            rhs=b_lines[:],
+                            start=True,
+                            stop=True,
+                        )
                     nc.scalar.copy(out=repeated[:, block * BLOCK : (block + 1) * BLOCK], in_=bank[:])
                 return repeated
 
-            def stand_on_partitions(gate, factor):
-                stood = keep.tile([P, HIDDEN // P], F32, name="bias_cols%d" % gate)
-                bank = psum.tile([P, BLOCK], F32, tag="bank")
-                spread = bank[:].rearrange("p (m n) -> p m n", n=SPREAD)
-                for m in range(HIDDEN // P):
-                    first = gate * HIDDEN + m * P
-                    nc.tensor.matmul(
-                        out=spread[:, m, :], lhsT=b_row[:, first : first + P], rhs=ones[:, 0:SPREAD], start=True, stop=True
-                    )
-                nc.vector.tensor_scalar_mul(out=stood[:], in0=spread[:, 0 : HIDDEN // P, 0], scalar1=factor)
-                return stood
-
-            for t in tiles:
-                quantise_rows(t)
             bias_f = repeat_on_partitions(GATE_F)
             bias_i = repeat_on_partitions(GATE_I)
-            bias_z = stand_on_partitions(GATE_Z, 1.0)
-            half_bias_o = stand_on_partitions(GATE_O, 0.5)
-            return bias_f, bias_i, bias_z, half_bias_o
+            stood = psum.tile([P, 2 * BLOCK], BF16, tag="bank")
+            nc.tensor.transpose(stood[:, 0:P], b_lines[:], identity_bf[:])
+            lines = HIDDEN // P
+            bias_z = keep.tile([P, lines], F32)
+            half_bias_o = keep.tile([P, lines], F32)
+            nc.vector.tensor_copy(out=bias_z[:], in_=stood[:, GATE_Z * lines : (GATE_Z + 1) * lines])
+            nc.vector.tensor_scalar_mul(
+                out=half_bias_o[:], in0=stood[:, GATE_O * lines : (GATE_O + 1) * lines], scalar1=0.5
+            )
 
-        with tc.tile_pool(name="stage", bufs=1) as stage:
-            bias_f, bias_i, bias_z, half_bias_o = load_and_prepare(stage)
-        results = ctx.enter_context(tc.tile_pool(name="results", bufs=BLOCKS * ROW_TILES))
+            def quantise_operand(operand, raw):
+                flipped, grouped = [], []
+                for t in tiles:
+                    words = raw[:, t, :].bitcast(F32)
+                    bank = psum.tile([P, BLOCK], F32, tag="bank")
+                    flipped.append(bank[:].rearrange("p (g u r) -> p g u r", g=OPERAND_PASSES, u=PAIRS))
+                    for g in range(OPERAND_PASSES):
+                        for u in range(PAIRS):
+                            nc.tensor.transpose(
+                                flipped[t][:, g, u, :],
+                                words[:, PASS_WORDS * g + u : PASS_WORDS * (g + 1) : PAIRS],
+                                identity[:],
+                            )
 
-        def gate_by_rows(gate, block, t, bias_rows, func, scale, name):
+                def interleave(t):
+                    grouped.append(stage.tile([P, OPERAND_PASSES, P, PACK], BF16, align_bytes=64, name="grouped%d_%d" % (operand, t)))
+                    target = grouped[t][:].bitcast(F32)
+                    source = flipped[t].rearrange("p g u r -> p g r u")
+                    if t % 2 == 0:
+                        nc.vector.tensor_copy(out=target, in_=source)
+                    else:
+                        nc.scalar.copy(out=target, in_=source)
+
+                def quantise(t):
+                    rows = slice(t * P, (t + 1) * P)
+                    for g in range(OPERAND_PASSES):
+                        s = OPERAND_PASSES * operand + g
+                        nc.vector.quantize_mx(
+                            out=a_codes[:, s, rows].bitcast(FP8X4),
+                            scales=a_planes[:, s, rows],
+                            in_=grouped[t][:, g, :, :].rearrange("p r k -> p (r k)"),
+                        )
+
+                for t in tiles:
+                    interleave(t)
+                    if t % 2 == 0:
+                        if t > 0:
+                            quantise(t - 1)
+                        quantise(t)
+                quantise(ROW_TILES - 1)
+
+            quantise_operand(0, x_raw)
+            f_banks = [psum.tile([P, BLOCK], F32, tag="bank", name="f_bank") for t in tiles]
+            for t in tiles:
+                passes_by_rows(f_banks[t], GATE_F, 0, t, range(OPERAND_PASSES))
+            quantise_operand(1, h_raw)
+            return bias_f, bias_i, bias_z, half_bias_o, f_banks
+
+        def weight_plane(s, pre_cols):
+            return w_planes[s // OPERAND_PASSES][PLANE_ROWS * (s % OPERAND_PASSES) : P, pre_cols]
+
+        def passes_by_rows(acc, gate, block, t, passes):
             pre_cols = slice(gate * HIDDEN + block * BLOCK, gate * HIDDEN + (block + 1) * BLOCK)
             rows = slice(t * P, (t + 1) * P)
-            acc = psum.tile([P, BLOCK], F32, tag="bank")
-            for s in range(PASSES):
+            for s in passes:
                 nc.tensor.matmul_mx(
                     out=acc[:],
                     lhsT=a_codes[:, s, rows].bitcast(FP8X4),
                     lhsT_scale=a_planes[:, s, rows],
                     rhs=w_codes[:, s, pre_cols].bitcast(FP8X4),
-                    rhs_scale=w_planes[PLANE_ROWS * s : P, pre_cols],
+                    rhs_scale=weight_plane(s, pre_cols),
                     start=(s == 0),
                     stop=(s == PASSES - 1),
                 )
-            value = gates.tile([P, BLOCK], F32, name=name)
-            nc.vector.tensor_tensor(
-                out=value[:], in0=acc[:], in1=bias_rows[:, block * BLOCK : (block + 1) * BLOCK], op=ALU.add
-            )
-            nc.scalar.activation(out=value[:], in_=value[:], func=func, scale=scale)
-            return value
 
-        def gate_by_columns(gate, block, bias_cols, scale, name):
-            values = []
-            for j in range(COL_TILES):
-                m = block * COL_TILES + j
-                pre_cols = slice(gate * HIDDEN + m * P, gate * HIDDEN + (m + 1) * P)
-                acc = psum.tile([P, BATCH], F32, tag="bank")
-                for s in range(PASSES):
-                    nc.tensor.matmul_mx(
-                        out=acc[:],
-                        lhsT=w_codes[:, s, pre_cols].bitcast(FP8X4),
-                        lhsT_scale=w_planes[PLANE_ROWS * s : P, pre_cols],
-                        rhs=a_codes[:, s, :].bitcast(FP8X4),
-                        rhs_scale=a_planes[:, s, :],
-                        start=(s == 0),
-                        stop=(s == PASSES - 1),
-                    )
-                value = gates.tile([P, BATCH], F32, name=name)
-                nc.scalar.activation(out=value[:], in_=acc[:], func=ACT.Tanh, bias=bias_cols[:, m : m + 1], scale=scale)
-                values.append(value)
-            return values
+        with tc.tile_pool(name="stage", bufs=1) as stage:
+            bias_f, bias_i, bias_z, half_bias_o, f_banks = load_and_prepare(stage)
+        results = ctx.enter_context(tc.tile_pool(name="results", bufs=BLOCKS * ROW_TILES))
+        once = ctx.enter_context(tc.tile_pool(name="once", bufs=1))
+        twice = ctx.enter_context(tc.tile_pool(name="twice", bufs=BLOCKS))
 
-        def rows_onto_partitions(values, name):
-            banks = [psum.tile([P, BLOCK], F32, tag="bank", name=name) for t in tiles]
-            for j, value in enumerate(values):
-                for t in tiles:
-                    nc.tensor.transpose(banks[t][:, j * P : (j + 1) * P], value[:, t * P : (t + 1) * P], identity[:])
-            return banks
+        def columns(block):
+            return slice(block * BLOCK, (block + 1) * BLOCK)
+
+        def j_cols(j):
+            return slice(j * P, (j + 1) * P)
+
+        def by_rows(gate, block, t, bias_rows, value, func, scale, acc=None):
+            if acc is None:
+                acc = psum.tile([P, BLOCK], F32, tag="bank")
+                passes_by_rows(acc, gate, block, t, range(PASSES))
+            else:
+                passes_by_rows(acc, gate, block, t, range(OPERAND_PASSES, PASSES))
+            nc.vector.tensor_tensor(out=value, in0=acc[:], in1=bias_rows[:, columns(block)], op=ALU.add)
+            nc.scalar.activation(out=value, in_=value, func=func, scale=scale)
 
         def f_gate(block):
-            return [gate_by_rows(GATE_F, block, t, bias_f, ACT.Tanh, 0.5, "tanh_f") for t in tiles]
-
-        def o_gate(block):
-            return gate_by_columns(GATE_O, block, half_bias_o, 0.5, "tanh_o_cols")
-
-        def finish_h(block, tanh_o_cols, half_ratio):
-            tanh_o = rows_onto_partitions(tanh_o_cols, "tanh_o")
+            values = []
             for t in tiles:
-                h_new = results.tile([P, BLOCK], F32, name="h_new")
-                nc.vector.scalar_tensor_tensor(
-                    out=h_new[:], in0=tanh_o[t][:], scalar=1.0, in1=half_ratio[t][:], op0=ALU.add, op1=ALU.mult
+                values.append(gates.tile([P, BLOCK], F32, name="tanh_f"))
+                by_rows(GATE_F, block, t, bias_f, values[t][:], ACT.Tanh, 0.5, acc=f_banks[t] if block == 0 else None)
+            return values
+
+        def column_tile(gate, block, j, bias_cols, scale, value):
+            m = block * COL_TILES + j
+            pre_cols = slice(gate * HIDDEN + m * P, gate * HIDDEN + (m + 1) * P)
+            acc = psum.tile([P, BATCH], F32, tag="bank")
+            for s in range(PASSES):
+                nc.tensor.matmul_mx(
+                    out=acc[:],
+                    lhsT=w_codes[:, s, pre_cols].bitcast(FP8X4),
+                    lhsT_scale=weight_plane(s, pre_cols),
+                    rhs=a_codes[:, s, :].bitcast(FP8X4),
+                    rhs_scale=a_planes[:, s, :],
+                    start=(s == 0),
+                    stop=(s == PASSES - 1),
                 )
-                nc.sync.dma_start(out=row_tiled(h_out)[:, t, block * BLOCK : (block + 1) * BLOCK], in_=h_new[:])
+            nc.scalar.activation(out=value, in_=acc[:], func=ACT.Tanh, bias=bias_cols[:, m : m + 1], scale=scale)
+
+        def turned(value):
+            bank = psum.tile([P, ROW_TILES, P], F32, tag="bank")
+            for t in tiles:
+                nc.tensor.transpose(bank[:, t, :], value[:, t * P : (t + 1) * P], identity[:])
+            return bank
+
+        def z_gate(block):
+            values = []
+            for j in range(COL_TILES):
+                values.append(gates.tile([P, BATCH], F32, name="z_cols"))
+                column_tile(GATE_Z, block, j, bias_z, 1.0, values[j][:])
+            return values
+
+        def o_gate(block, js):
+            values = []
+            for j in js:
+                values.append(results.tile([P, BATCH], F32, name="tanh_o_cols"))
+                column_tile(GATE_O, block, j, half_bias_o, 0.5, values[-1][:])
+            return values
+
+        def halve_n(block):
+            nc.vector.tensor_scalar_mul(out=n_half[:, :, columns(block)], in0=n_old[:, :, columns(block)], scalar1=0.5)
+
+        def f_n(block, t):
+            n_new[block].append(results.tile([P, BLOCK], F32, name="n_new"))
+            nc.vector.scalar_tensor_tensor(
+                out=n_new[block][t][:], in0=tanh_f[t][:], scalar=1.0, in1=n_half[:, t, columns(block)], op0=ALU.add, op1=ALU.mult
+            )
+
+        def f_c(block, t):
+            c_new[block].append(results.tile([P, BLOCK], F32, name="c_new"))
+            nc.vector.scalar_tensor_tensor(
+                out=c_new[block][t][:], in0=tanh_f[t][:], scalar=1.0, in1=c_old[:, t, columns(block)], op0=ALU.add, op1=ALU.mult
+            )
+
+        def finish_n(block, t):
+            nc.vector.scalar_tensor_tensor(
+                out=n_new[block][t][:], in0=exp_i[:, t, :], scalar=I_MAX, in1=n_new[block][t][:], op0=ALU.min, op1=ALU.add
+            )
+            nc.sync.dma_start(out=row_tiled(n_out)[:, t, columns(block)], in_=n_new[block][t][:])
+
+        def logarithm(block):
+            inverse[block] = twice.tile([P, ROW_TILES, BLOCK], F32, name="inverse")
+            for t in tiles:
+                nc.scalar.activation(
+                    out=inverse[block][:, t, :], in_=n_new[block][t][:], func=ACT.Ln, bias=two_eps[:], scale=2.0
+                )
+
+        def invert(block):
+            for t in tiles:
+                nc.scalar.activation(out=inverse[block][:, t, :], in_=inverse[block][:, t, :], func=ACT.Exp, scale=-1.0)
+
+        def finish_c(block, z_cols):
+            banks = [turned(value) for value in z_cols]
+            for j in range(COL_TILES):
+                nc.vector.scalar_tensor_tensor(
+                    out=iz[:, :, j_cols(j)], in0=exp_i[:, :, j_cols(j)], scalar=I_MAX, in1=banks[j][:], op0=ALU.min, op1=ALU.mult
+                )
+            for t in tiles:
+                nc.vector.scalar_tensor_tensor(
+                    out=c_new[block][t][:], in0=c_new[block][t][:], scalar=0.5, in1=iz[:, t, :], op0=ALU.mult, op1=ALU.add
+                )
+                nc.sync.dma_start(out=row_tiled(c_out)[:, t, columns(block)], in_=c_new[block][t][:])
+
+        def half_ratio(block, t, engine):
+            engine.tensor_tensor(
+                out=inverse[block][:, t, :], in0=c_new[block][t][:], in1=inverse[block][:, t, :], op=ALU.mult
+            )
+
+        def finish_h(block, tanh_o_cols):
+            for j in range(COL_TILES):
+                bank = turned(tanh_o_cols[j])
+                h_new = results.tile([P, ROW_TILES, P], F32, name="h_new")
+                nc.vector.scalar_tensor_tensor(
+                    out=h_new[:], in0=bank[:], scalar=1.0, in1=inverse[block][:, :, j_cols(j)], op0=ALU.add, op1=ALU.mult
+                )
+                first = block * BLOCK + j * P
+                nc.sync.dma_start(out=row_tiled(h_out)[:, :, first : first + P], in_=h_new[:])
+
+        n_new, c_new, inverse = ([], []), ([], []), [None, None]
+        exp_i = once.tile([P, ROW_TILES, BLOCK], F32)
+        iz = once.tile([P, ROW_TILES, BLOCK], F32)
 
         tanh_f = f_gate(0)
-        for block in range(BLOCKS):
-            cols = slice(block * BLOCK, (block + 1) * BLOCK)
-            c_new, n_new, iz, inverse = [], [], [], []
-            z_cols = gate_by_columns(GATE_Z, block, bias_z, 1.0, "z_cols")
-            nc.vector.tensor_scalar_mul(out=n_half[:, :, cols], in0=n_old[:, :, cols], scalar1=0.5)
-            for t in tiles:
-                c_new.append(results.tile([P, BLOCK], F32, name="c_new"))
-                n_new.append(results.tile([P, BLOCK], F32, name="n_new"))
-                nc.vector.scalar_tensor_tensor(
-                    out=n_new[t][:], in0=tanh_f[t][:], scalar=1.0, in1=n_half[:, t, cols], op0=ALU.add, op1=ALU.mult
-                )
-                nc.vector.scalar_tensor_tensor(
-                    out=c_new[t][:], in0=tanh_f[t][:], scalar=1.0, in1=c_old[:, t, cols], op0=ALU.add, op1=ALU.mult
-                )
-            if block > 0:
-                tanh_o_cols = o_gate(block - 1)
-            exp_i = [gate_by_rows(GATE_I, block, t, bias_i, ACT.Exp, 1.0, "exp_i") for t in tiles]
-            z = rows_onto_partitions(z_cols, "z")
-            for t in tiles:
-                nc.vector.scalar_tensor_tensor(
-                    out=n_new[t][:], in0=exp_i[t][:], scalar=I_MAX, in1=n_new[t][:], op0=ALU.min, op1=ALU.add
-                )
-                nc.sync.dma_start(out=row_tiled(n_out)[:, t, cols], in_=n_new[t][:])
-                inverse.append(gates.tile([P, BLOCK], F32, name="inverse"))
-                nc.scalar.activation(out=inverse[t][:], in_=n_new[t][:], func=ACT.Ln, bias=two_eps[:], scale=2.0)
-            for t in tiles:
-                iz.append(gates.tile([P, BLOCK], F32, name="iz"))
-                nc.vector.scalar_tensor_tensor(
-                    out=iz[t][:], in0=exp_i[t][:], scalar=I_MAX, in1=z[t][:], op0=ALU.min, op1=ALU.mult
-                )
-            for t in tiles:
-                nc.vector.scalar_tensor_tensor(
-                    out=c_new[t][:], in0=c_new[t][:], scalar=0.5, in1=iz[t][:], op0=ALU.mult, op1=ALU.add
-                )
-                nc.sync.dma_start(out=row_tiled(c_out)[:, t, cols], in_=c_new[t][:])
-            for t in tiles:
-                nc.scalar.activation(out=inverse[t][:], in_=inverse[t][:], func=ACT.Exp, scale=-1.0)
-            if block > 0:
-                finish_h(block - 1, tanh_o_cols, half_ratio)
-            if block + 1 < BLOCKS:
-                tanh_f = f_gate(block + 1)
-            half_ratio = [gates.tile([P, BLOCK], F32, name="half_ratio") for t in tiles]
-            for t in tiles:
-                engine = nc.gpsimd if t >= ROW_TILES - ON_GPSIMD else nc.vector
-                engine.tensor_tensor(out=half_ratio[t][:], in0=c_new[t][:], in1=inverse[t][:], op=ALU.mult)
-        finish_h(BLOCKS - 1, o_gate(BLOCKS - 1), half_ratio)
+        halve_n(0)
+        for t in tiles:
+            by_rows(GATE_I, 0, t, bias_i, exp_i[:, t, :], ACT.Exp, 1.0)
+            f_n(0, t)
+        z_cols = z_gate(0)
+        for t in tiles:
+            finish_n(0, t)
+        for t in tiles:
+            f_c(0, t)
+        logarithm(0)
+        tanh_f = f_gate(1)
+        finish_c(0, z_cols)
+        invert(0)
+        for t in tiles:
+            half_ratio(0, t, nc.gpsimd)
+        halve_n(1)
+        for t in tiles:
+            by_rows(GATE_I, 1, t, bias_i, exp_i[:, t, :], ACT.Exp, 1.0)
+        for t in tiles:
+            f_n(1, t)
+        for t in tiles:
+            finish_n(1, t)
+        for t in tiles:
+            f_c(1, t)
+        logarithm(1)
+        z_cols = z_gate(1)
+        tanh_o_0 = o_gate(0, range(COL_TILES))
+        invert(1)
+        finish_c(1, z_cols)
+        tanh_o_1 = o_gate(1, range(COL_TILES // 2))
+        for t in range(ROW_TILES - ON_GPSIMD):
+            half_ratio(1, t, nc.gpsimd)
+        finish_h(0, tanh_o_0)
+        tanh_o_1 += o_gate(1, range(COL_TILES // 2, COL_TILES))
+        for t in range(ROW_TILES - ON_GPSIMD, ROW_TILES):
+            half_ratio(1, t, nc.vector)
+        finish_h(1, tanh_o_1)

@@ -94,36 +94,32 @@ def tile_slstmcell_kernel(
                 nc.sync.dma_start(out=n_old[:, :, cols], in_=row_tiled(n_prev)[:, :, cols])
                 nc.sync.dma_start(out=c_old[:, :, cols], in_=row_tiled(c_prev)[:, :, cols])
 
-            def load_scales(operand, first_gate, last_gate):
+            def load_scales(operand, first_gate, last_gate, queue, view):
                 cols = slice(first_gate * HIDDEN, (last_gate + 1) * HIDDEN)
                 scales = (W_scales, R_scales)[operand]
                 for quadrant in range(QUADRANTS):
                     top = QUADRANT * quadrant
-                    nc.sync.dma_start(
-                        out=w_planes[operand][top : top + OPERAND_PASSES * PLANE_ROWS, cols].bitcast(I32),
-                        in_=scales[:, PLANE_ROWS * quadrant : PLANE_ROWS * (quadrant + 1), cols].bitcast(I32),
+                    queue.dma_start(
+                        out=w_planes[operand][top : top + OPERAND_PASSES * PLANE_ROWS, cols].bitcast(view),
+                        in_=scales[:, PLANE_ROWS * quadrant : PLANE_ROWS * (quadrant + 1), cols].bitcast(view),
                     )
 
             nc.sync.dma_start(out=x_raw[:], in_=row_tiled(x_t))
-            load_scales(0, GATE_F, GATE_F)
+            load_scales(0, GATE_F, GATE_F, nc.sync, I32)
             load_weights(0, GATE_F, 0)
             nc.sync.dma_start(out=h_raw[:], in_=row_tiled(h_prev))
-            load_scales(1, GATE_F, GATE_F)
+            load_scales(1, GATE_F, GATE_F, nc.sync, I32)
             load_weights(1, GATE_F, 0)
-            def load_both_scales(gate):
+            for first_gate, last_gate in ((GATE_Z, GATE_I), (GATE_O, GATE_O)):
                 for operand in range(2):
-                    load_scales(operand, gate, gate)
-
-            load_both_scales(GATE_I)
+                    load_scales(operand, first_gate, last_gate, nc.gpsimd, F32)
             load_weight_block(GATE_I, 0)
             load_state_block(0)
-            load_both_scales(GATE_Z)
             load_weight_block(GATE_Z, 0)
             load_weight_block(GATE_F, 1)
             load_state_block(1)
             load_weight_block(GATE_I, 1)
             load_weight_block(GATE_Z, 1)
-            load_both_scales(GATE_O)
             for block in range(BLOCKS):
                 load_weight_block(GATE_O, block)
 

@@ -110,15 +110,17 @@ def tile_slstmcell_kernel(
             nc.sync.dma_start(out=h_raw[:], in_=row_tiled(h_prev))
             load_scales(1, GATE_F, GATE_F, nc.sync, I32)
             load_weights(1, GATE_F, 0)
-            for first_gate, last_gate in ((GATE_Z, GATE_I), (GATE_O, GATE_O)):
+            for gate in (GATE_Z, GATE_O):
                 for operand in range(2):
-                    load_scales(operand, first_gate, last_gate, nc.gpsimd, F32)
+                    load_scales(operand, gate, gate, nc.gpsimd, F32)
+            load_weight_block(GATE_F, 1)
+            for operand in range(2):
+                load_scales(operand, GATE_I, GATE_I, nc.sync, I32)
             load_weight_block(GATE_I, 0)
             load_state_block(0)
             load_weight_block(GATE_Z, 0)
-            load_weight_block(GATE_F, 1)
-            load_state_block(1)
             load_weight_block(GATE_I, 1)
+            load_state_block(1)
             load_weight_block(GATE_Z, 1)
             for block in range(BLOCKS):
                 load_weight_block(GATE_O, block)
@@ -240,7 +242,7 @@ def tile_slstmcell_kernel(
         def f_gate(block):
             values = []
             for t in tiles:
-                values.append(gates.tile([P, BLOCK], F32, name="tanh_f"))
+                values.append(gates.tile([P, BLOCK], F32, name="tanh_f%d" % block))
                 by_rows(GATE_F, block, t, bias_f, values[t][:], ACT.Tanh, 0.5, acc=f_banks[t] if block == 0 else None)
             return values
 
@@ -286,18 +288,18 @@ def tile_slstmcell_kernel(
         def f_n(block, t):
             n_new[block].append(results.tile([P, BLOCK], F32, name="n_new"))
             nc.vector.scalar_tensor_tensor(
-                out=n_new[block][t][:], in0=tanh_f[t][:], scalar=1.0, in1=n_half[:, t, columns(block)], op0=ALU.add, op1=ALU.mult
+                out=n_new[block][t][:], in0=tanh_f[block][t][:], scalar=1.0, in1=n_half[:, t, columns(block)], op0=ALU.add, op1=ALU.mult
             )
 
         def f_c(block, t):
             c_new[block].append(results.tile([P, BLOCK], F32, name="c_new"))
             nc.vector.scalar_tensor_tensor(
-                out=c_new[block][t][:], in0=tanh_f[t][:], scalar=1.0, in1=c_old[:, t, columns(block)], op0=ALU.add, op1=ALU.mult
+                out=c_new[block][t][:], in0=tanh_f[block][t][:], scalar=1.0, in1=c_old[:, t, columns(block)], op0=ALU.add, op1=ALU.mult
             )
 
         def finish_n(block, t):
             nc.vector.scalar_tensor_tensor(
-                out=n_new[block][t][:], in0=exp_i[:, t, :], scalar=I_MAX, in1=n_new[block][t][:], op0=ALU.min, op1=ALU.add
+                out=n_new[block][t][:], in0=exp_i[block][:, t, :], scalar=I_MAX, in1=n_new[block][t][:], op0=ALU.min, op1=ALU.add
             )
             nc.sync.dma_start(out=row_tiled(n_out)[:, t, columns(block)], in_=n_new[block][t][:])
 
@@ -312,12 +314,14 @@ def tile_slstmcell_kernel(
             for t in tiles:
                 nc.scalar.activation(out=inverse[block][:, t, :], in_=inverse[block][:, t, :], func=ACT.Exp, scale=-1.0)
 
-        def finish_c(block, z_cols):
+        def i_z(block, z_cols):
             banks = [turned(value) for value in z_cols]
             for j in range(COL_TILES):
                 nc.vector.scalar_tensor_tensor(
-                    out=iz[:, :, j_cols(j)], in0=exp_i[:, :, j_cols(j)], scalar=I_MAX, in1=banks[j][:], op0=ALU.min, op1=ALU.mult
+                    out=iz[:, :, j_cols(j)], in0=exp_i[block][:, :, j_cols(j)], scalar=I_MAX, in1=banks[j][:], op0=ALU.min, op1=ALU.mult
                 )
+
+        def finish_c(block):
             for t in tiles:
                 nc.vector.scalar_tensor_tensor(
                     out=c_new[block][t][:], in0=c_new[block][t][:], scalar=0.5, in1=iz[:, t, :], op0=ALU.mult, op1=ALU.add
@@ -340,39 +344,40 @@ def tile_slstmcell_kernel(
                 nc.sync.dma_start(out=row_tiled(h_out)[:, :, first : first + P], in_=h_new[:])
 
         n_new, c_new, inverse = ([], []), ([], []), [None, None]
-        exp_i = once.tile([P, ROW_TILES, BLOCK], F32)
+        exp_i = [twice.tile([P, ROW_TILES, BLOCK], F32, name="exp_i") for block in range(BLOCKS)]
         iz = once.tile([P, ROW_TILES, BLOCK], F32)
 
-        tanh_f = f_gate(0)
+        tanh_f = [f_gate(block) for block in range(BLOCKS)]
         halve_n(0)
         for t in tiles:
-            by_rows(GATE_I, 0, t, bias_i, exp_i[:, t, :], ACT.Exp, 1.0)
+            by_rows(GATE_I, 0, t, bias_i, exp_i[0][:, t, :], ACT.Exp, 1.0)
             f_n(0, t)
-        z_cols = z_gate(0)
         for t in tiles:
             finish_n(0, t)
-        for t in tiles:
-            f_c(0, t)
         logarithm(0)
-        tanh_f = f_gate(1)
-        finish_c(0, z_cols)
-        invert(0)
-        for t in tiles:
-            half_ratio(0, t, nc.gpsimd)
+        z_cols = z_gate(0)
         halve_n(1)
-        for t in tiles:
-            by_rows(GATE_I, 1, t, bias_i, exp_i[:, t, :], ACT.Exp, 1.0)
         for t in tiles:
             f_n(1, t)
         for t in tiles:
+            f_c(0, t)
+        for t in tiles:
+            by_rows(GATE_I, 1, t, bias_i, exp_i[1][:, t, :], ACT.Exp, 1.0)
+        i_z(0, z_cols)
+        for t in tiles:
             finish_n(1, t)
+        finish_c(0)
         for t in tiles:
             f_c(1, t)
+        invert(0)
+        for t in tiles:
+            half_ratio(0, t, nc.gpsimd)
         logarithm(1)
         z_cols = z_gate(1)
         tanh_o_0 = o_gate(0, range(COL_TILES))
         invert(1)
-        finish_c(1, z_cols)
+        i_z(1, z_cols)
+        finish_c(1)
         tanh_o_1 = o_gate(1, range(COL_TILES // 2))
         for t in range(ROW_TILES - ON_GPSIMD):
             half_ratio(1, t, nc.gpsimd)

@@ -68,6 +68,8 @@ def tile_slstmcell_kernel(
             x_raw = stage.tile([P, ROW_TILES, HIDDEN], BF16)
             h_raw = stage.tile([P, ROW_TILES, HIDDEN], BF16)
 
+            zeros = stage.tile([P, BLOCK], BF16)
+            nc.vector.memset(zeros[:].bitcast(I32), 0)
             nc.gpsimd.memset(b_lines[:].bitcast(I32), 0)
             nc.sync.dma_start(out=b_lines[0 : GATES * HIDDEN // P, :], in_=b.rearrange("(m p) -> m p", p=P))
             make_identity(nc, identity[:])
@@ -125,6 +127,13 @@ def tile_slstmcell_kernel(
             for block in range(BLOCKS):
                 load_weight_block(GATE_O, block)
 
+            def idle_matmuls(count):
+                bank = psum.tile([P, BLOCK], F32, tag="bank", name="idle")
+                for repeat in range(count):
+                    nc.tensor.matmul(out=bank[:], lhsT=zeros[:, 0:P], rhs=zeros[:], start=True, stop=True)
+
+            idle_matmuls(6)
+
             def repeat_on_partitions(gate):
                 repeated = keep.tile([P, HIDDEN], BF16, name="bias_rows%d" % gate)
                 for block in range(BLOCKS):
@@ -156,6 +165,8 @@ def tile_slstmcell_kernel(
             def quantise_operand(operand, raw):
                 flipped, grouped = [], []
                 for t in tiles:
+                    if t % 2 == 1:
+                        idle_matmuls(1)
                     words = raw[:, t, :].bitcast(F32)
                     bank = psum.tile([P, BLOCK], F32, tag="bank")
                     flipped.append(bank[:].rearrange("p (g u r) -> p g u r", g=OPERAND_PASSES, u=PAIRS))

@@ -106,7 +106,9 @@ def tile_slstmcell_kernel(
                         in_=scales[:, PLANE_ROWS * quadrant : PLANE_ROWS * (quadrant + 1), cols].bitcast(view),
                     )
 
-            nc.sync.dma_start(out=x_raw[:], in_=row_tiled(x_t))
+            half = ROW_TILES // 2
+            for first in (0, half):
+                nc.sync.dma_start(out=x_raw[:, first : first + half, :], in_=row_tiled(x_t)[:, first : first + half, :])
             load_scales(0, GATE_F, GATE_F, nc.sync, I32)
             load_weights(0, GATE_F, 0)
             nc.sync.dma_start(out=h_raw[:], in_=row_tiled(h_prev))
@@ -132,7 +134,7 @@ def tile_slstmcell_kernel(
                 for repeat in range(count):
                     nc.tensor.matmul(out=bank[:], lhsT=zeros[:, 0:P], rhs=zeros[:], start=True, stop=True)
 
-            idle_matmuls(6)
+            idle_matmuls(4)
 
             def repeat_on_partitions(gate):
                 repeated = keep.tile([P, HIDDEN], BF16, name="bias_rows%d" % gate)
@@ -151,38 +153,27 @@ def tile_slstmcell_kernel(
                 return repeated
 
             bias_f = repeat_on_partitions(GATE_F)
-            bias_i = repeat_on_partitions(GATE_I)
-            stood = psum.tile([P, 2 * BLOCK], BF16, tag="bank")
-            nc.tensor.transpose(stood[:, 0:P], b_lines[:], identity_bf[:])
-            lines = HIDDEN // P
-            bias_z = keep.tile([P, lines], F32)
-            half_bias_o = keep.tile([P, lines], F32)
-            nc.vector.tensor_copy(out=bias_z[:], in_=stood[:, GATE_Z * lines : (GATE_Z + 1) * lines])
-            nc.vector.tensor_scalar_mul(
-                out=half_bias_o[:], in0=stood[:, GATE_O * lines : (GATE_O + 1) * lines], scalar1=0.5
-            )
 
             def quantise_operand(operand, raw):
                 flipped, grouped = [], []
                 for t in tiles:
                     if t % 2 == 1:
                         idle_matmuls(1)
-                    words = raw[:, t, :].bitcast(F32)
+                    words = stage.tile([P, OPERAND_PASSES, PAIRS, P], F32, name="words%d_%d" % (operand, t))
+                    nc.vector.tensor_copy(
+                        out=words[:], in_=raw[:, t, :].bitcast(F32).rearrange("p (g q u) -> p g u q", g=OPERAND_PASSES, u=PAIRS)
+                    )
                     bank = psum.tile([P, BLOCK], F32, tag="bank")
                     flipped.append(bank[:].rearrange("p (g u r) -> p g u r", g=OPERAND_PASSES, u=PAIRS))
                     for g in range(OPERAND_PASSES):
                         for u in range(PAIRS):
-                            nc.tensor.transpose(
-                                flipped[t][:, g, u, :],
-                                words[:, PASS_WORDS * g + u : PASS_WORDS * (g + 1) : PAIRS],
-                                identity[:],
-                            )
+                            nc.tensor.transpose(flipped[t][:, g, u, :], words[:, g, u, :], identity[:])
 
                 def interleave(t):
                     grouped.append(stage.tile([P, OPERAND_PASSES, P, PACK], BF16, align_bytes=64, name="grouped%d_%d" % (operand, t)))
                     target = grouped[t][:].bitcast(F32)
                     source = flipped[t].rearrange("p g u r -> p g r u")
-                    if t % 2 == 0:
+                    if operand == 1 and t % 2 == 0:
                         nc.vector.tensor_copy(out=target, in_=source)
                     else:
                         nc.scalar.copy(out=target, in_=source)
@@ -206,6 +197,17 @@ def tile_slstmcell_kernel(
                 quantise(ROW_TILES - 1)
 
             quantise_operand(0, x_raw)
+            bias_i = repeat_on_partitions(GATE_I)
+            stood = psum.tile([P, 2 * BLOCK], BF16, tag="bank")
+            nc.tensor.transpose(stood[:, 0:P], b_lines[:], identity_bf[:])
+            lines = HIDDEN // P
+            bias_z = keep.tile([P, lines], F32)
+            half_bias_o = keep.tile([P, lines], F32)
+            nc.vector.tensor_copy(out=bias_z[:], in_=stood[:, GATE_Z * lines : (GATE_Z + 1) * lines])
+            nc.vector.tensor_scalar_mul(
+                out=half_bias_o[:], in0=stood[:, GATE_O * lines : (GATE_O + 1) * lines], scalar1=0.5
+            )
+
             f_banks = [psum.tile([P, BLOCK], F32, tag="bank", name="f_bank") for t in tiles]
             for t in tiles:
                 passes_by_rows(f_banks[t], GATE_F, 0, t, range(OPERAND_PASSES))

from contextlib import ExitStack

import concourse.mybir as mybir
from concourse.masks import make_identity

FP8X4 = mybir.dt.float8_e4m3fn_x4
BF16 = mybir.dt.bfloat16
F32 = mybir.dt.float32
I32 = mybir.dt.int32
U32 = mybir.dt.uint32
U8 = mybir.dt.uint8
ACT = mybir.ActivationFunctionType
ALU = mybir.AluOpType

P = 128
PSUM_BANKS = 8
BATCH = 512
HIDDEN = 1024
GATES = 4
GATE_Z, GATE_I, GATE_F, GATE_O = 0, 1, 2, 3
PACK = 4
K_PASS = P * PACK
OPERAND_PASSES = HIDDEN // K_PASS
PASSES = 2 * OPERAND_PASSES
PAIRS = PACK // 2
PASS_WORDS = K_PASS // 2
QUADRANT = 32
QUADRANTS = P // QUADRANT
PLANE_ROWS = 4
ROW_TILES = BATCH // P
BLOCK = 512
BLOCKS = HIDDEN // BLOCK
COL_TILES = BLOCK // P
EPS = 1e-6
I_MAX = 50.0
ON_GPSIMD = 2

FLOPS = 2 * BATCH * (2 * HIDDEN) * (GATES * HIDDEN)


def tile_slstmcell_kernel(
    tc, x_t, h_prev, c_prev, n_prev, W_words, W_scales, R_words, R_scales, b, h_out, c_out, n_out
):
    nc = tc.nc
    tiles = range(ROW_TILES)
    with ExitStack() as ctx:
        ctx.enter_context(tc.manual_schedule())
        keep = ctx.enter_context(tc.tile_pool(name="keep", bufs=1))
        psum = ctx.enter_context(tc.psum_pool(name="psum", bufs=PSUM_BANKS))
        gates = ctx.enter_context(tc.tile_pool(name="gates", bufs=ROW_TILES))

        w_codes = keep.tile([P, PASSES, GATES * HIDDEN], U32, align_bytes=64)
        a_codes = keep.tile([P, PASSES, BATCH], U32, align_bytes=64)
        w_planes = [keep.tile([P, GATES * HIDDEN], U8, align_bytes=64, name="planes%d" % operand) for operand in range(2)]
        a_planes = keep.tile([P, PASSES, BATCH], U8, align_bytes=64)
        c_old = keep.tile([P, ROW_TILES, HIDDEN], BF16)
        n_old = keep.tile([P, ROW_TILES, HIDDEN], BF16)
        n_half = keep.tile([P, ROW_TILES, HIDDEN], BF16)
        identity = keep.tile([P, P], F32)
        two_eps = keep.tile([P, 1], F32)

        def row_tiled(dram):
            return dram.rearrange("(p t) d -> p t d", t=ROW_TILES)

        def load_and_prepare(stage):
            b_lines = stage.tile([P, P], BF16)
            identity_bf = stage.tile([P, P], BF16)
            x_raw = stage.tile([P, ROW_TILES, HIDDEN], BF16)
            h_raw = stage.tile([P, ROW_TILES, HIDDEN], BF16)

            zeros = stage.tile([P, BLOCK], BF16)
            nc.vector.memset(zeros[:].bitcast(I32), 0)
            nc.gpsimd.memset(b_lines[:].bitcast(I32), 0)
            nc.sync.dma_start(out=b_lines[0 : GATES * HIDDEN // P, :], in_=b.rearrange("(m p) -> m p", p=P))
            make_identity(nc, identity[:])
            nc.vector.tensor_copy(out=identity_bf[:], in_=identity[:])
            nc.vector.memset(w_planes[0][:].bitcast(I32), 0)
            nc.gpsimd.memset(w_planes[1][:].bitcast(I32), 0)
            nc.vector.memset(two_eps[:], 2.0 * EPS)

            def load_weights(operand, gate, block):
                first = gate * HIDDEN + block * BLOCK
                passes = slice(OPERAND_PASSES * operand, OPERAND_PASSES * (operand + 1))
                words = (W_words, R_words)[operand]
                nc.sync.dma_start(
                    out=w_codes[:, passes, first : first + BLOCK].bitcast(I32),
                    in_=words.rearrange("g p n t -> p g (n t)")[:, :, PACK * first : PACK * (first + BLOCK)].bitcast(I32),
                )

            def load_weight_block(gate, block):
                for operand in range(2):
                    load_weights(operand, gate, block)

            def load_state_block(block):
                cols = slice(block * BLOCK, (block + 1) * BLOCK)
                nc.sync.dma_start(out=n_old[:, :, cols], in_=row_tiled(n_prev)[:, :, cols])
                nc.sync.dma_start(out=c_old[:, :, cols], in_=row_tiled(c_prev)[:, :, cols])

            def load_scales(operand, first_gate, last_gate, queue, view):
                cols = slice(first_gate * HIDDEN, (last_gate + 1) * HIDDEN)
                scales = (W_scales, R_scales)[operand]
                for quadrant in range(QUADRANTS):
                    top = QUADRANT * quadrant
                    queue.dma_start(
                        out=w_planes[operand][top : top + OPERAND_PASSES * PLANE_ROWS, cols].bitcast(view),
                        in_=scales[:, PLANE_ROWS * quadrant : PLANE_ROWS * (quadrant + 1), cols].bitcast(view),
                    )

            half = ROW_TILES // 2
            for first in (0, half):
                nc.sync.dma_start(out=x_raw[:, first : first + half, :], in_=row_tiled(x_t)[:, first : first + half, :])
            load_scales(0, GATE_F, GATE_F, nc.sync, I32)
            load_weights(0, GATE_F, 0)
            nc.sync.dma_start(out=h_raw[:], in_=row_tiled(h_prev))
            load_scales(1, GATE_F, GATE_F, nc.sync, I32)
            load_weights(1, GATE_F, 0)
            for gate in (GATE_Z, GATE_O):
                for operand in range(2):
                    load_scales(operand, gate, gate, nc.gpsimd, F32)
            load_weight_block(GATE_F, 1)
            for operand in range(2):
                load_scales(operand, GATE_I, GATE_I, nc.sync, I32)
            load_weight_block(GATE_I, 0)
            load_state_block(0)
            load_weight_block(GATE_Z, 0)
            load_weight_block(GATE_I, 1)
            load_state_block(1)
            load_weight_block(GATE_Z, 1)
            for block in range(BLOCKS):
                load_weight_block(GATE_O, block)

            def idle_matmuls(count):
                bank = psum.tile([P, BLOCK], F32, tag="bank", name="idle")
                for repeat in range(count):
                    nc.tensor.matmul(out=bank[:], lhsT=zeros[:, 0:P], rhs=zeros[:], start=True, stop=True)

            idle_matmuls(4)

            def repeat_on_partitions(gate):
                repeated = keep.tile([P, HIDDEN], BF16, name="bias_rows%d" % gate)
                for block in range(BLOCKS):
                    bank = psum.tile([P, BLOCK], F32, tag="bank")
                    for j in range(COL_TILES):
                        m = (gate * HIDDEN + block * BLOCK) // P + j
                        nc.tensor.matmul(
                            out=bank[:, j * P : (j + 1) * P],
                            lhsT=identity_bf[:, m : m + 1].to_broadcast([P, P]),
                            rhs=b_lines[:],
                            start=True,
                            stop=True,
                        )
                    nc.scalar.copy(out=repeated[:, block * BLOCK : (block + 1) * BLOCK], in_=bank[:])
                return repeated

            bias_f = repeat_on_partitions(GATE_F)

            def quantise_operand(operand, raw):
                flipped, grouped = [], []
                for t in tiles:
                    if t % 2 == 1:
                        idle_matmuls(1)
                    words = stage.tile([P, OPERAND_PASSES, PAIRS, P], F32, name="words%d_%d" % (operand, t))
                    nc.vector.tensor_copy(
                        out=words[:], in_=raw[:, t, :].bitcast(F32).rearrange("p (g q u) -> p g u q", g=OPERAND_PASSES, u=PAIRS)
                    )
                    bank = psum.tile([P, BLOCK], F32, tag="bank")
                    flipped.append(bank[:].rearrange("p (g u r) -> p g u r", g=OPERAND_PASSES, u=PAIRS))
                    for g in range(OPERAND_PASSES):
                        for u in range(PAIRS):
                            nc.tensor.transpose(flipped[t][:, g, u, :], words[:, g, u, :], identity[:])

                def interleave(t):
                    grouped.append(stage.tile([P, OPERAND_PASSES, P, PACK], BF16, align_bytes=64, name="grouped%d_%d" % (operand, t)))
                    target = grouped[t][:].bitcast(F32)
                    source = flipped[t].rearrange("p g u r -> p g r u")
                    if operand == 1 and t % 2 == 0:
                        nc.vector.tensor_copy(out=target, in_=source)
                    else:
                        nc.scalar.copy(out=target, in_=source)

                def quantise(t):
                    rows = slice(t * P, (t + 1) * P)
                    for g in range(OPERAND_PASSES):
                        s = OPERAND_PASSES * operand + g
                        nc.vector.quantize_mx(
                            out=a_codes[:, s, rows].bitcast(FP8X4),
                            scales=a_planes[:, s, rows],
                            in_=grouped[t][:, g, :, :].rearrange("p r k -> p (r k)"),
                        )

                for t in tiles:
                    interleave(t)
                    if t % 2 == 0:
                        if t > 0:
                            quantise(t - 1)
                        quantise(t)
                quantise(ROW_TILES - 1)

            quantise_operand(0, x_raw)
            bias_i = repeat_on_partitions(GATE_I)
            stood = psum.tile([P, 2 * BLOCK], BF16, tag="bank")
            nc.tensor.transpose(stood[:, 0:P], b_lines[:], identity_bf[:])
            lines = HIDDEN // P
            bias_z = keep.tile([P, lines], F32)
            half_bias_o = keep.tile([P, lines], F32)
            nc.vector.tensor_copy(out=bias_z[:], in_=stood[:, GATE_Z * lines : (GATE_Z + 1) * lines])
            nc.vector.tensor_scalar_mul(
                out=half_bias_o[:], in0=stood[:, GATE_O * lines : (GATE_O + 1) * lines], scalar1=0.5
            )

            f_banks = [psum.tile([P, BLOCK], F32, tag="bank", name="f_bank") for t in tiles]
            for t in tiles:
                passes_by_rows(f_banks[t], GATE_F, 0, t, range(OPERAND_PASSES))
            quantise_operand(1, h_raw)
            return bias_f, bias_i, bias_z, half_bias_o, f_banks

        def weight_plane(s, pre_cols):
            return w_planes[s // OPERAND_PASSES][PLANE_ROWS * (s % OPERAND_PASSES) : P, pre_cols]

        def passes_by_rows(acc, gate, block, t, passes):
            pre_cols = slice(gate * HIDDEN + block * BLOCK, gate * HIDDEN + (block + 1) * BLOCK)
            rows = slice(t * P, (t + 1) * P)
            for s in passes:
                nc.tensor.matmul_mx(
                    out=acc[:],
                    lhsT=a_codes[:, s, rows].bitcast(FP8X4),
                    lhsT_scale=a_planes[:, s, rows],
                    rhs=w_codes[:, s, pre_cols].bitcast(FP8X4),
                    rhs_scale=weight_plane(s, pre_cols),
                    start=(s == 0),
                    stop=(s == PASSES - 1),
                )

        with tc.tile_pool(name="stage", bufs=1) as stage:
            bias_f, bias_i, bias_z, half_bias_o, f_banks = load_and_prepare(stage)
        results = ctx.enter_context(tc.tile_pool(name="results", bufs=BLOCKS * ROW_TILES))
        once = ctx.enter_context(tc.tile_pool(name="once", bufs=1))
        twice = ctx.enter_context(tc.tile_pool(name="twice", bufs=BLOCKS))

        def columns(block):
            return slice(block * BLOCK, (block + 1) * BLOCK)

        def j_cols(j):
            return slice(j * P, (j + 1) * P)

        def by_rows(gate, block, t, bias_rows, value, func, scale, acc=None):
            if acc is None:
                acc = psum.tile([P, BLOCK], F32, tag="bank")
                passes_by_rows(acc, gate, block, t, range(PASSES))
            else:
                passes_by_rows(acc, gate, block, t, range(OPERAND_PASSES, PASSES))
            nc.vector.tensor_tensor(out=value, in0=acc[:], in1=bias_rows[:, columns(block)], op=ALU.add)
            nc.scalar.activation(out=value, in_=value, func=func, scale=scale)

        def f_gate(block):
            values = []
            for t in tiles:
                values.append(gates.tile([P, BLOCK], F32, name="tanh_f%d" % block))
                by_rows(GATE_F, block, t, bias_f, values[t][:], ACT.Tanh, 0.5, acc=f_banks[t] if block == 0 else None)
            return values

        def column_tile(gate, block, j, bias_cols, scale, value):
            m = block * COL_TILES + j
            pre_cols = slice(gate * HIDDEN + m * P, gate * HIDDEN + (m + 1) * P)
            acc = psum.tile([P, BATCH], F32, tag="bank")
            for s in range(PASSES):
                nc.tensor.matmul_mx(
                    out=acc[:],
                    lhsT=w_codes[:, s, pre_cols].bitcast(FP8X4),
                    lhsT_scale=weight_plane(s, pre_cols),
                    rhs=a_codes[:, s, :].bitcast(FP8X4),
                    rhs_scale=a_planes[:, s, :],
                    start=(s == 0),
                    stop=(s == PASSES - 1),
                )
            nc.scalar.activation(out=value, in_=acc[:], func=ACT.Tanh, bias=bias_cols[:, m : m + 1], scale=scale)

        def turned(value):
            bank = psum.tile([P, ROW_TILES, P], F32, tag="bank")
            for t in tiles:
                nc.tensor.transpose(bank[:, t, :], value[:, t * P : (t + 1) * P], identity[:])
            return bank

        def z_gate(block):
            values = []
            for j in range(COL_TILES):
                values.append(gates.tile([P, BATCH], F32, name="z_cols"))
                column_tile(GATE_Z, block, j, bias_z, 1.0, values[j][:])
            return values

        def o_gate(block, js):
            values = []
            for j in js:
                values.append(results.tile([P, BATCH], F32, name="tanh_o_cols"))
                column_tile(GATE_O, block, j, half_bias_o, 0.5, values[-1][:])
            return values

        def halve_n(block):
            nc.vector.tensor_scalar_mul(out=n_half[:, :, columns(block)], in0=n_old[:, :, columns(block)], scalar1=0.5)

        def f_n(block, t):
            n_new[block].append(results.tile([P, BLOCK], F32, name="n_new"))
            nc.vector.scalar_tensor_tensor(
                out=n_new[block][t][:], in0=tanh_f[block][t][:], scalar=1.0, in1=n_half[:, t, columns(block)], op0=ALU.add, op1=ALU.mult
            )

        def f_c(block, t):
            c_new[block].append(results.tile([P, BLOCK], F32, name="c_new"))
            nc.vector.scalar_tensor_tensor(
                out=c_new[block][t][:], in0=tanh_f[block][t][:], scalar=1.0, in1=c_old[:, t, columns(block)], op0=ALU.add, op1=ALU.mult
            )

        def finish_n(block, t):
            nc.vector.scalar_tensor_tensor(
                out=n_new[block][t][:], in0=exp_i[block][:, t, :], scalar=I_MAX, in1=n_new[block][t][:], op0=ALU.min, op1=ALU.add
            )
            nc.sync.dma_start(out=row_tiled(n_out)[:, t, columns(block)], in_=n_new[block][t][:])

        def logarithm(block):
            inverse[block] = twice.tile([P, ROW_TILES, BLOCK], F32, name="inverse")
            for t in tiles:
                nc.scalar.activation(
                    out=inverse[block][:, t, :], in_=n_new[block][t][:], func=ACT.Ln, bias=two_eps[:], scale=2.0
                )

        def invert(block):
            for t in tiles:
                nc.scalar.activation(out=inverse[block][:, t, :], in_=inverse[block][:, t, :], func=ACT.Exp, scale=-1.0)

        def i_z(block, z_cols):
            banks = [turned(value) for value in z_cols]
            for j in range(COL_TILES):
                nc.vector.scalar_tensor_tensor(
                    out=iz[:, :, j_cols(j)], in0=exp_i[block][:, :, j_cols(j)], scalar=I_MAX, in1=banks[j][:], op0=ALU.min, op1=ALU.mult
                )

        def finish_c(block):
            for t in tiles:
                nc.vector.scalar_tensor_tensor(
                    out=c_new[block][t][:], in0=c_new[block][t][:], scalar=0.5, in1=iz[:, t, :], op0=ALU.mult, op1=ALU.add
                )
                nc.sync.dma_start(out=row_tiled(c_out)[:, t, columns(block)], in_=c_new[block][t][:])

        def half_ratio(block, t, engine):
            engine.tensor_tensor(
                out=inverse[block][:, t, :], in0=c_new[block][t][:], in1=inverse[block][:, t, :], op=ALU.mult
            )

        def finish_h(block, tanh_o_cols):
            for j in range(COL_TILES):
                bank = turned(tanh_o_cols[j])
                h_new = results.tile([P, ROW_TILES, P], F32, name="h_new")
                nc.vector.scalar_tensor_tensor(
                    out=h_new[:], in0=bank[:], scalar=1.0, in1=inverse[block][:, :, j_cols(j)], op0=ALU.add, op1=ALU.mult
                )
                first = block * BLOCK + j * P
                nc.sync.dma_start(out=row_tiled(h_out)[:, :, first : first + P], in_=h_new[:])

        n_new, c_new, inverse = ([], []), ([], []), [None, None]
        exp_i = [twice.tile([P, ROW_TILES, BLOCK], F32, name="exp_i") for block in range(BLOCKS)]
        iz = once.tile([P, ROW_TILES, BLOCK], F32)

        tanh_f = [f_gate(block) for block in range(BLOCKS)]
        halve_n(0)
        for t in tiles:
            by_rows(GATE_I, 0, t, bias_i, exp_i[0][:, t, :], ACT.Exp, 1.0)
            f_n(0, t)
        for t in tiles:
            finish_n(0, t)
        logarithm(0)
        z_cols = z_gate(0)
        halve_n(1)
        for t in tiles:
            f_n(1, t)
        for t in tiles:
            f_c(0, t)
        for t in tiles:
            by_rows(GATE_I, 1, t, bias_i, exp_i[1][:, t, :], ACT.Exp, 1.0)
        i_z(0, z_cols)
        for t in tiles:
            finish_n(1, t)
        finish_c(0)
        for t in tiles:
            f_c(1, t)
        invert(0)
        for t in tiles:
            half_ratio(0, t, nc.gpsimd)
        logarithm(1)
        z_cols = z_gate(1)
        tanh_o_0 = o_gate(0, range(COL_TILES))
        invert(1)
        i_z(1, z_cols)
        finish_c(1)
        tanh_o_1 = o_gate(1, range(COL_TILES // 2))
        for t in range(ROW_TILES - ON_GPSIMD):
            half_ratio(1, t, nc.gpsimd)
        finish_h(0, tanh_o_0)
        tanh_o_1 += o_gate(1, range(COL_TILES // 2, COL_TILES))
        for t in range(ROW_TILES - ON_GPSIMD, ROW_TILES):
            half_ratio(1, t, nc.vector)
        finish_h(1, tanh_o_1)
